import numpy as np
import ml_dtypes


def mxq(x, axis, fmt="e4m3"):
    dtype, down = {"e4m3": (ml_dtypes.float8_e4m3fn, 7), "e5m2": (ml_dtypes.float8_e5m2, 14)}[fmt]
    v = np.moveaxis(np.asarray(x, np.float32).astype(ml_dtypes.bfloat16).astype(np.float64), axis, -1)
    blocks = v.reshape(v.shape[:-1] + (-1, 32))
    amax = np.abs(blocks).max(-1, keepdims=True)
    byte = np.maximum(np.where(amax > 0, np.frexp(amax)[1] - 1 + 127, 0) - down, 1)
    scale = np.exp2(byte - 127.0)
    codes = (blocks / scale).astype(np.float32).astype(dtype).astype(np.float64)
    return np.moveaxis((codes * scale).reshape(v.shape), -1, axis)


WIDE = False


def mx_kscale(k):
    if not WIDE:
        return np.ones(k)
    levels = np.array([10, -10, 5, -5, 0])
    a = np.random.permutation(np.resize(levels, k // 512 * 4)).reshape(k // 512, 4)
    idx = np.arange(k)
    return np.exp2(a[idx // 512, idx % 128 // 32])


BF16 = ml_dtypes.bfloat16


def bf(x):
    return np.asarray(x, np.float32).astype(BF16)


def f64(x):
    return np.asarray(x).astype(np.float64)


B, T, STOCH, ACT, HID, DETER, G = 4, 64, 1024, 512, 512, 4096, 8
N = B * T
BH = DETER // G


def silu(v):
    return v / (1.0 + np.exp(-v))


def sigmoid(v):
    return 1.0 / (1.0 + np.exp(-v))


def setup_inputs():
    t = mx_kscale(DETER)
    return {
        "h": bf(silu(np.random.standard_normal((N, DETER))) * t),
        "d": bf(np.random.standard_normal((B, T, DETER))),
        "W_gate": bf(np.random.standard_normal((G, BH, 3 * BH)) * 2.0 / np.sqrt(BH) / t.reshape(G, BH)[:, :, None]),
        "b_gate": bf(0.3 * np.random.standard_normal((G, 3 * BH))),
    }


def reference(h, d, W_gate, b_gate):
    hq = mxq(f64(h).reshape(N, G, BH).transpose(1, 0, 2), 2, "e4m3")
    gates = (hq @ mxq(f64(W_gate), 1, "e4m3")) + f64(b_gate)[:, None, :]
    gates = gates.transpose(1, 0, 2)
    reset, update, cand = np.split(gates, 3, axis=-1)
    reset = sigmoid(reset.reshape(N, DETER))
    update = sigmoid(update.reshape(N, DETER) - 1.0)
    cand = np.tanh(reset * cand.reshape(N, DETER))
    d2 = f64(d).reshape(N, DETER)
    return (update * cand + (1.0 - update) * d2).reshape(B, T, DETER)

@@ -1,0 +1,241 @@
+from contextlib import ExitStack
+
+import concourse.mybir as mybir
+from concourse.masks import make_identity
+
+FP8X4 = mybir.dt.float8_e4m3fn_x4
+BF16 = mybir.dt.bfloat16
+F32 = mybir.dt.float32
+U32 = mybir.dt.uint32
+U8 = mybir.dt.uint8
+ACT = mybir.ActivationFunctionType
+ALU = mybir.AluOpType
+
+P = 128
+PACK = 4
+ROWS = 256
+ROW_TILES = ROWS // P
+BLOCKS = 8
+BLOCK = 512
+GATES = 3
+RESET = 0
+UPDATE = 1
+CAND = 2
+UNIT = 256
+UNIT_TILES = UNIT // P
+UNITS = BLOCKS * BLOCK // UNIT
+UNITS_PER_BLOCK = BLOCK // UNIT
+BIAS_TILES = BLOCKS * GATES * BLOCK // P
+RUN = 4
+
+FLOPS = 2 * ROWS * BLOCKS * BLOCK * GATES * BLOCK
+
+
+def tile_blockrecurrentmodel_pb_kernel(tc, h, d, W_gate, b_gate, out):
+    nc = tc.nc
+
+    h_view = h.rearrange("(r p) (g f) -> g p r f", p=P, f=BLOCK)
+    d_view = d.flatten_outer_dims().rearrange("(r p) (g f) -> g p r f", p=P, f=BLOCK)
+    out_view = out.flatten_outer_dims().rearrange("(r p) (i f) -> i p r f", p=P, f=UNIT)
+    w_view = W_gate.rearrange("g (p t) c -> g p t c", t=PACK)
+    bias_view = b_gate.rearrange("g (m p) -> (g m) p", p=P)
+
+    with ExitStack() as ctx:
+        ctx.enter_context(tc.manual_schedule())
+        const = ctx.enter_context(tc.tile_pool(name="const", bufs=1))
+        inputs = ctx.enter_context(tc.tile_pool(name="inputs", bufs=BLOCKS))
+        stage = ctx.enter_context(tc.tile_pool(name="stage", bufs=2))
+        quant = ctx.enter_context(tc.tile_pool(name="quant", bufs=3))
+        work = ctx.enter_context(tc.tile_pool(name="work", bufs=2))
+        psum = ctx.enter_context(tc.psum_pool(name="psum", bufs=1))
+
+        bias_rows = const.tile([P, P], BF16)
+        nc.scalar.dma_start(out=bias_rows[0:BIAS_TILES, :], in_=bias_view)
+        h_tiles, w_tiles, d_tiles = [], [], []
+        for g in range(BLOCKS):
+            h_sb = inputs.tile([P, ROW_TILES, BLOCK], BF16)
+            nc.sync.dma_start(out=h_sb[:], in_=h_view[g])
+            w_sb = inputs.tile([P, PACK, GATES * BLOCK], BF16)
+            pieces = GATES if g == 0 else 1
+            width = GATES * BLOCK // pieces
+            for s in range(pieces):
+                cols = slice(s * width, (s + 1) * width)
+                nc.sync.dma_start(out=w_sb[:, :, cols], in_=w_view[g][:, :, cols])
+            d_sb = inputs.tile([P, ROW_TILES, BLOCK], BF16)
+            nc.sync.dma_start(out=d_sb[:], in_=d_view[g])
+            h_tiles.append(h_sb)
+            w_tiles.append(w_sb)
+            d_tiles.append(d_sb)
+
+        ident_f32 = const.tile([P, P], F32)
+        make_identity(nc, ident_f32[:])
+        ident_bf16 = const.tile([P, P], BF16)
+        make_identity(nc, ident_bf16[:])
+
+        zero = const.tile([P, 1], F32)
+        nc.vector.memset(zero[:], 0.0)
+        warm = const.tile([P, 1], F32)
+        nc.scalar.activation(out=warm[:], in_=zero[:], func=ACT.Sigmoid)
+
+        nc.vector.memset(bias_rows[BIAS_TILES:P, :], 0.0)
+        bias_turned = psum.tile([P, P], BF16, tag="h_turned")
+        nc.tensor.transpose(bias_turned[:], bias_rows[:], ident_bf16[:])
+        bias = const.tile([P, BIAS_TILES], F32)
+        nc.vector.tensor_copy(out=bias[:], in_=bias_turned[:, 0:BIAS_TILES])
+        update_bias = bias[:].rearrange("p (g a q) -> p g a q", g=BLOCKS, a=GATES)[:, :, UPDATE, :]
+        nc.vector.tensor_scalar_add(out=update_bias, in0=update_bias, scalar1=-1.0)
+
+        def bias_column(i, gate, j):
+            g, part = divmod(i, UNITS_PER_BLOCK)
+            col = (g * GATES + gate) * (BLOCK // P) + part * UNIT_TILES + j
+            return bias[:, col : col + 1]
+
+        h_grouped, h_codes, h_scales = {}, {}, {}
+        w_grouped, w_codes, w_scales = {}, {}, {}
+        gates, d_turned, out_turned = {}, {}, {}
+
+        def turn_h(g):
+            words = h_tiles[g][:].rearrange("p r f -> p (r f)").bitcast(F32)
+            words = words.rearrange("p (r q u) -> p r u q", r=ROW_TILES, u=2)
+            turned = psum.tile([P, 2, ROWS], F32, tag="h_turned")
+            for u in range(2):
+                for r in range(ROW_TILES):
+                    nc.tensor.transpose(turned[:, u, r * P : (r + 1) * P], words[:, r, u, :], ident_f32[:])
+            grouped = stage.tile([P, ROWS * PACK], BF16, align_bytes=64, tag="h_grouped")
+            nc.vector.tensor_copy(
+                out=grouped[:].bitcast(F32).rearrange("p (n u) -> p n u", u=2),
+                in_=turned[:].rearrange("p u n -> p n u"),
+            )
+            h_grouped[g] = grouped
+
+        def quantise_h(g):
+            codes = quant.tile([P, ROWS], U32, align_bytes=64, tag="h_codes")
+            scales = quant.tile([P, ROWS], U8, align_bytes=64, tag="h_scales")
+            nc.vector.quantize_mx(out=codes[:].bitcast(FP8X4), scales=scales[:], in_=h_grouped[g][:])
+            h_codes[g], h_scales[g] = codes, scales
+
+        def regroup_weights(i):
+            g, part = divmod(i, UNITS_PER_BLOCK)
+            grouped = stage.tile([P, GATES * UNIT, PACK], BF16, align_bytes=64, tag="w_grouped")
+            for gate in range(GATES):
+                first = gate * BLOCK + part * UNIT
+                src = w_tiles[g][:, :, first : first + UNIT].rearrange("p t (c s) -> p c t s", s=RUN)
+                dst = grouped[:, gate * UNIT : (gate + 1) * UNIT, :].rearrange("p (c s) t -> p c t s", s=RUN)
+                if gate == CAND:
+                    nc.vector.tensor_copy(out=dst, in_=src)
+                else:
+                    nc.scalar.copy(out=dst, in_=src)
+            w_grouped[i] = grouped
+
+        def quantise_weights(i):
+            codes = quant.tile([P, GATES * UNIT], U32, align_bytes=64, tag="w_codes")
+            scales = quant.tile([P, GATES * UNIT], U8, align_bytes=64, tag="w_scales")
+            flat = w_grouped[i][:].rearrange("p w t -> p (w t)")
+            for lo, hi in ((0, 2 * UNIT), (2 * UNIT, 3 * UNIT)):
+                nc.vector.quantize_mx(
+                    out=codes[:, lo:hi].bitcast(FP8X4),
+                    scales=scales[:, lo:hi],
+                    in_=flat[:, lo * PACK : hi * PACK],
+                )
+            w_codes[i], w_scales[i] = codes, scales
+
+        def multiply(i):
+            g = i // UNITS_PER_BLOCK
+            banks = []
+            for gate, tag in ((RESET, "r"), (UPDATE, "u"), (CAND, "c")):
+                bank = psum.tile([P, UNIT_TILES, ROWS], F32, tag=tag)
+                for j in range(UNIT_TILES):
+                    cols = slice(gate * UNIT + j * P, gate * UNIT + (j + 1) * P)
+                    nc.tensor.matmul_mx(
+                        out=bank[:, j, :],
+                        lhsT=w_codes[i][:, cols].bitcast(FP8X4),
+                        lhsT_scale=w_scales[i][:, cols],
+                        rhs=h_codes[g][:].bitcast(FP8X4),
+                        rhs_scale=h_scales[g][:],
+                        start=True,
+                        stop=True,
+                    )
+                banks.append(bank)
+            gates[i] = banks
+
+        def turn_d(i):
+            g, part = divmod(i, UNITS_PER_BLOCK)
+            turned = psum.tile([P, UNIT_TILES, ROWS], BF16, tag="d_turned", bufs=2)
+            for j in range(UNIT_TILES):
+                first = part * UNIT + j * P
+                for r in range(ROW_TILES):
+                    nc.tensor.transpose(
+                        turned[:, j, r * P : (r + 1) * P], d_tiles[g][:, r, first : first + P], ident_bf16[:]
+                    )
+            d_turned[i] = turned
+
+        def add_d_and_store(i):
+            g, part = divmod(i, UNITS_PER_BLOCK)
+            result = work.tile([P, ROW_TILES, UNIT], F32, tag="result", bufs=3)
+            nc.vector.tensor_tensor(
+                out=result[:],
+                in0=out_turned[i][:],
+                in1=d_tiles[g][:, :, part * UNIT : (part + 1) * UNIT],
+                op=ALU.add,
+            )
+            nc.sync.dma_start(out=out_view[i], in_=result[:])
+
+        turn_h(0)
+        regroup_weights(0)
+        regroup_weights(1)
+        quantise_h(0)
+        quantise_weights(0)
+        multiply(0)
+        turn_d(0)
+
+        for i in range(UNITS):
+            g, part = divmod(i, UNITS_PER_BLOCK)
+            r_bank, u_bank, c_bank = gates[i]
+
+            reset = work.tile([P, UNIT_TILES, ROWS], F32, tag="reset")
+            update = work.tile([P, UNIT_TILES, ROWS], F32, tag="update")
+            for gate, bank, act in ((RESET, r_bank, reset), (UPDATE, u_bank, update)):
+                for j in range(UNIT_TILES):
+                    nc.scalar.activation(
+                        out=act[:, j, :], in_=bank[:, j, :], func=ACT.Sigmoid, bias=bias_column(i, gate, j)
+                    )
+            gated = work.tile([P, UNIT_TILES, ROWS], F32, tag="gated")
+            for j in range(UNIT_TILES):
+                nc.vector.scalar_tensor_tensor(
+                    out=gated[:, j, :],
+                    in0=c_bank[:, j, :],
+                    scalar=bias_column(i, CAND, j),
+                    in1=reset[:, j, :],
+                    op0=ALU.add,
+                    op1=ALU.mult,
+                )
+            cand = work.tile([P, UNIT_TILES, ROWS], F32, tag="cand")
+            nc.scalar.activation(out=cand[:], in_=gated[:], func=ACT.Tanh)
+
+            if i + 1 < UNITS:
+                if part == UNITS_PER_BLOCK - 1:
+                    quantise_h(g + 1)
+                quantise_weights(i + 1)
+                multiply(i + 1)
+                turn_d(i + 1)
+            if i >= 1:
+                add_d_and_store(i - 1)
+
+            diff = work.tile([P, UNIT_TILES, ROWS], F32, tag="diff")
+            nc.vector.tensor_tensor(out=diff[:], in0=cand[:], in1=d_turned[i][:], op=ALU.subtract)
+            step = work.tile([P, UNIT_TILES, ROWS], F32, tag="step")
+            nc.vector.tensor_tensor(out=step[:], in0=update[:], in1=diff[:], op=ALU.mult)
+            turned = psum.tile([P, ROW_TILES, UNIT], F32, tag="out_turned", bufs=2)
+            for r in range(ROW_TILES):
+                for j in range(UNIT_TILES):
+                    nc.tensor.transpose(
+                        turned[:, r, j * P : (j + 1) * P], step[:, j, r * P : (r + 1) * P], ident_f32[:]
+                    )
+            out_turned[i] = turned
+
+            if i + 2 < UNITS:
+                regroup_weights(i + 2)
+            if part == 0 and g + 1 < BLOCKS:
+                turn_h(g + 1)
+
+        add_d_and_store(UNITS - 1)

@@ -90,9 +90,10 @@ def tile_blockrecurrentmodel_pb_kernel(tc, h, d, W_gate, b_gate, out):
             col = (g * GATES + gate) * (BLOCK // P) + part * UNIT_TILES + j
             return bias[:, col : col + 1]
 
-        h_grouped, h_codes, h_scales = {}, {}, {}
+        h_turned, h_grouped, h_codes, h_scales = {}, {}, {}, {}
         w_grouped, w_codes, w_scales = {}, {}, {}
         gates, d_turned, out_turned = {}, {}, {}
+        reset, update, gated, cand = {}, {}, {}, {}
 
         def turn_h(g):
             words = h_tiles[g][:].rearrange("p r f -> p (r f)").bitcast(F32)
@@ -101,10 +102,13 @@ def tile_blockrecurrentmodel_pb_kernel(tc, h, d, W_gate, b_gate, out):
             for u in range(2):
                 for r in range(ROW_TILES):
                     nc.tensor.transpose(turned[:, u, r * P : (r + 1) * P], words[:, r, u, :], ident_f32[:])
+            h_turned[g] = turned
+
+        def group_h(g):
             grouped = stage.tile([P, ROWS * PACK], BF16, align_bytes=64, tag="h_grouped")
             nc.vector.tensor_copy(
                 out=grouped[:].bitcast(F32).rearrange("p (n u) -> p n u", u=2),
-                in_=turned[:].rearrange("p u n -> p n u"),
+                in_=h_turned[g][:].rearrange("p u n -> p n u"),
             )
             h_grouped[g] = grouped
 
@@ -169,6 +173,49 @@ def tile_blockrecurrentmodel_pb_kernel(tc, h, d, W_gate, b_gate, out):
                     )
             d_turned[i] = turned
 
+        def sigmoids(i):
+            r_bank, u_bank, c_bank = gates[i]
+            reset_sb = work.tile([P, UNIT_TILES, ROWS], F32, tag="reset")
+            update_sb = work.tile([P, UNIT_TILES, ROWS], F32, tag="update")
+            for gate, bank, act in ((RESET, r_bank, reset_sb), (UPDATE, u_bank, update_sb)):
+                for j in range(UNIT_TILES):
+                    nc.scalar.activation(
+                        out=act[:, j, :], in_=bank[:, j, :], func=ACT.Sigmoid, bias=bias_column(i, gate, j)
+                    )
+            reset[i], update[i] = reset_sb, update_sb
+
+        def gate_candidate(i):
+            r_bank, u_bank, c_bank = gates[i]
+            gated_sb = work.tile([P, UNIT_TILES, ROWS], F32, tag="gated")
+            for j in range(UNIT_TILES):
+                nc.vector.scalar_tensor_tensor(
+                    out=gated_sb[:, j, :],
+                    in0=c_bank[:, j, :],
+                    scalar=bias_column(i, CAND, j),
+                    in1=reset[i][:, j, :],
+                    op0=ALU.add,
+                    op1=ALU.mult,
+                )
+            gated[i] = gated_sb
+
+        def candidate(i):
+            cand_sb = work.tile([P, UNIT_TILES, ROWS], F32, tag="cand")
+            nc.scalar.activation(out=cand_sb[:], in_=gated[i][:], func=ACT.Tanh)
+            cand[i] = cand_sb
+
+        def blend(i):
+            diff = work.tile([P, UNIT_TILES, ROWS], F32, tag="diff")
+            nc.vector.tensor_tensor(out=diff[:], in0=cand[i][:], in1=d_turned[i][:], op=ALU.subtract)
+            step = work.tile([P, UNIT_TILES, ROWS], F32, tag="step")
+            nc.vector.tensor_tensor(out=step[:], in0=update[i][:], in1=diff[:], op=ALU.mult)
+            turned = psum.tile([P, ROW_TILES, UNIT], F32, tag="out_turned", bufs=2)
+            for r in range(ROW_TILES):
+                for j in range(UNIT_TILES):
+                    nc.tensor.transpose(
+                        turned[:, r, j * P : (j + 1) * P], step[:, j, r * P : (r + 1) * P], ident_f32[:]
+                    )
+            out_turned[i] = turned
+
         def add_d_and_store(i):
             g, part = divmod(i, UNITS_PER_BLOCK)
             result = work.tile([P, ROW_TILES, UNIT], F32, tag="result", bufs=3)
@@ -180,62 +227,31 @@ def tile_blockrecurrentmodel_pb_kernel(tc, h, d, W_gate, b_gate, out):
             )
             nc.sync.dma_start(out=out_view[i], in_=result[:])
 
-        turn_h(0)
-        regroup_weights(0)
-        regroup_weights(1)
-        quantise_h(0)
-        quantise_weights(0)
-        multiply(0)
-        turn_d(0)
+        def exists(i):
+            return 0 <= i < UNITS
 
-        for i in range(UNITS):
-            g, part = divmod(i, UNITS_PER_BLOCK)
-            r_bank, u_bank, c_bank = gates[i]
-
-            reset = work.tile([P, UNIT_TILES, ROWS], F32, tag="reset")
-            update = work.tile([P, UNIT_TILES, ROWS], F32, tag="update")
-            for gate, bank, act in ((RESET, r_bank, reset), (UPDATE, u_bank, update)):
-                for j in range(UNIT_TILES):
-                    nc.scalar.activation(
-                        out=act[:, j, :], in_=bank[:, j, :], func=ACT.Sigmoid, bias=bias_column(i, gate, j)
-                    )
-            gated = work.tile([P, UNIT_TILES, ROWS], F32, tag="gated")
-            for j in range(UNIT_TILES):
-                nc.vector.scalar_tensor_tensor(
-                    out=gated[:, j, :],
-                    in0=c_bank[:, j, :],
-                    scalar=bias_column(i, CAND, j),
-                    in1=reset[:, j, :],
-                    op0=ALU.add,
-                    op1=ALU.mult,
-                )
-            cand = work.tile([P, UNIT_TILES, ROWS], F32, tag="cand")
-            nc.scalar.activation(out=cand[:], in_=gated[:], func=ACT.Tanh)
-
-            if i + 1 < UNITS:
-                if part == UNITS_PER_BLOCK - 1:
-                    quantise_h(g + 1)
-                quantise_weights(i + 1)
-                multiply(i + 1)
-                turn_d(i + 1)
-            if i >= 1:
-                add_d_and_store(i - 1)
-
-            diff = work.tile([P, UNIT_TILES, ROWS], F32, tag="diff")
-            nc.vector.tensor_tensor(out=diff[:], in0=cand[:], in1=d_turned[i][:], op=ALU.subtract)
-            step = work.tile([P, UNIT_TILES, ROWS], F32, tag="step")
-            nc.vector.tensor_tensor(out=step[:], in0=update[:], in1=diff[:], op=ALU.mult)
-            turned = psum.tile([P, ROW_TILES, UNIT], F32, tag="out_turned", bufs=2)
-            for r in range(ROW_TILES):
-                for j in range(UNIT_TILES):
-                    nc.tensor.transpose(
-                        turned[:, r, j * P : (j + 1) * P], step[:, j, r * P : (r + 1) * P], ident_f32[:]
-                    )
-            out_turned[i] = turned
-
-            if i + 2 < UNITS:
-                regroup_weights(i + 2)
-            if part == 0 and g + 1 < BLOCKS:
-                turn_h(g + 1)
-
-        add_d_and_store(UNITS - 1)
+        for t in range(-3, UNITS + 1):
+            if exists(t + 1):
+                sigmoids(t + 1)
+            if exists(t + 2):
+                quantise_weights(t + 2)
+                if (t + 2) % UNITS_PER_BLOCK == 0:
+                    quantise_h((t + 2) // UNITS_PER_BLOCK)
+            if exists(t + 1):
+                gate_candidate(t + 1)
+            if exists(t + 2):
+                multiply(t + 2)
+            if exists(t + 3) and (t + 3) % UNITS_PER_BLOCK == 0:
+                turn_h((t + 3) // UNITS_PER_BLOCK)
+            if exists(t + 1):
+                turn_d(t + 1)
+            if exists(t):
+                candidate(t)
+            if exists(t - 1):
+                add_d_and_store(t - 1)
+            if exists(t):
+                blend(t)
+            if exists(t + 3):
+                if (t + 3) % UNITS_PER_BLOCK == 0:
+                    group_h((t + 3) // UNITS_PER_BLOCK)
+                regroup_weights(t + 3)

@@ -41,7 +41,6 @@ def tile_blockrecurrentmodel_pb_kernel(tc, h, d, W_gate, b_gate, out):
     bias_view = b_gate.rearrange("g (m p) -> (g m) p", p=P)
 
     with ExitStack() as ctx:
-        ctx.enter_context(tc.manual_schedule())
         const = ctx.enter_context(tc.tile_pool(name="const", bufs=1))
         inputs = ctx.enter_context(tc.tile_pool(name="inputs", bufs=BLOCKS))
         stage = ctx.enter_context(tc.tile_pool(name="stage", bufs=2))

@@ -27,6 +27,7 @@ UNITS = BLOCKS * BLOCK // UNIT
 UNITS_PER_BLOCK = BLOCK // UNIT
 BIAS_TILES = BLOCKS * GATES * BLOCK // P
 RUN = 4
+CAND_COLUMNS_ON_SCALAR = 96
 
 FLOPS = 2 * ROWS * BLOCKS * BLOCK * GATES * BLOCK
 
@@ -43,7 +44,7 @@ def tile_blockrecurrentmodel_pb_kernel(tc, h, d, W_gate, b_gate, out):
     with ExitStack() as ctx:
         const = ctx.enter_context(tc.tile_pool(name="const", bufs=1))
         inputs = ctx.enter_context(tc.tile_pool(name="inputs", bufs=BLOCKS))
-        stage = ctx.enter_context(tc.tile_pool(name="stage", bufs=2))
+        stage = ctx.enter_context(tc.tile_pool(name="stage", bufs=3))
         quant = ctx.enter_context(tc.tile_pool(name="quant", bufs=3))
         work = ctx.enter_context(tc.tile_pool(name="work", bufs=2))
         psum = ctx.enter_context(tc.psum_pool(name="psum", bufs=1))
@@ -105,7 +106,7 @@ def tile_blockrecurrentmodel_pb_kernel(tc, h, d, W_gate, b_gate, out):
 
         def group_h(g):
             grouped = stage.tile([P, ROWS * PACK], BF16, align_bytes=64, tag="h_grouped")
-            nc.vector.tensor_copy(
+            nc.scalar.copy(
                 out=grouped[:].bitcast(F32).rearrange("p (n u) -> p n u", u=2),
                 in_=h_turned[g][:].rearrange("p u n -> p n u"),
             )
@@ -122,12 +123,26 @@ def tile_blockrecurrentmodel_pb_kernel(tc, h, d, W_gate, b_gate, out):
             grouped = stage.tile([P, GATES * UNIT, PACK], BF16, align_bytes=64, tag="w_grouped")
             for gate in range(GATES):
                 first = gate * BLOCK + part * UNIT
-                src = w_tiles[g][:, :, first : first + UNIT].rearrange("p t (c s) -> p c t s", s=RUN)
-                dst = grouped[:, gate * UNIT : (gate + 1) * UNIT, :].rearrange("p (c s) t -> p c t s", s=RUN)
-                if gate == CAND:
-                    nc.vector.tensor_copy(out=dst, in_=src)
+                piece = w_tiles[g][:, :, first : first + UNIT]
+                place = grouped[:, gate * UNIT : (gate + 1) * UNIT, :]
+                if gate == RESET:
+                    nc.gpsimd.tensor_scalar(
+                        out=place,
+                        in0=piece.rearrange("p t w -> p w t"),
+                        scalar1=1.0,
+                        scalar2=0.0,
+                        op0=ALU.mult,
+                        op1=ALU.add,
+                    )
                 else:
-                    nc.scalar.copy(out=dst, in_=src)
+                    src = piece.rearrange("p t (c s) -> p c t s", s=RUN)
+                    dst = place.rearrange("p (c s) t -> p c t s", s=RUN)
+                    if gate == UPDATE:
+                        nc.scalar.copy(out=dst, in_=src)
+                    else:
+                        cut = CAND_COLUMNS_ON_SCALAR // RUN
+                        nc.scalar.copy(out=dst[:, :cut], in_=src[:, :cut])
+                        nc.vector.tensor_copy(out=dst[:, cut:], in_=src[:, cut:])
             w_grouped[i] = grouped
 
         def quantise_weights(i):

@@ -28,6 +28,7 @@ UNITS_PER_BLOCK = BLOCK // UNIT
 BIAS_TILES = BLOCKS * GATES * BLOCK // P
 RUN = 4
 CAND_COLUMNS_ON_SCALAR = 96
+GPSIMD_COLUMNS = 128
 
 FLOPS = 2 * ROWS * BLOCKS * BLOCK * GATES * BLOCK
 
@@ -126,14 +127,15 @@ def tile_blockrecurrentmodel_pb_kernel(tc, h, d, W_gate, b_gate, out):
                 piece = w_tiles[g][:, :, first : first + UNIT]
                 place = grouped[:, gate * UNIT : (gate + 1) * UNIT, :]
                 if gate == RESET:
-                    nc.gpsimd.tensor_scalar(
-                        out=place,
-                        in0=piece.rearrange("p t w -> p w t"),
-                        scalar1=1.0,
-                        scalar2=0.0,
-                        op0=ALU.mult,
-                        op1=ALU.add,
-                    )
+                    for lo in range(0, UNIT, GPSIMD_COLUMNS):
+                        nc.gpsimd.tensor_scalar(
+                            out=place[:, lo : lo + GPSIMD_COLUMNS, :],
+                            in0=piece[:, :, lo : lo + GPSIMD_COLUMNS].rearrange("p t w -> p w t"),
+                            scalar1=1.0,
+                            scalar2=0.0,
+                            op0=ALU.mult,
+                            op1=ALU.add,
+                        )
                 else:
                     src = piece.rearrange("p t (c s) -> p c t s", s=RUN)
                     dst = place.rearrange("p (c s) t -> p c t s", s=RUN)
@@ -219,9 +221,15 @@ def tile_blockrecurrentmodel_pb_kernel(tc, h, d, W_gate, b_gate, out):
 
         def blend(i):
             diff = work.tile([P, UNIT_TILES, ROWS], F32, tag="diff")
-            nc.vector.tensor_tensor(out=diff[:], in0=cand[i][:], in1=d_turned[i][:], op=ALU.subtract)
             step = work.tile([P, UNIT_TILES, ROWS], F32, tag="step")
-            nc.vector.tensor_tensor(out=step[:], in0=update[i][:], in1=diff[:], op=ALU.mult)
+            for j in range(UNIT_TILES):
+                nc.vector.tensor_tensor(
+                    out=diff[:, j, :], in0=cand[i][:, j, :], in1=d_turned[i][:, j, :], op=ALU.subtract
+                )
+            for j in range(UNIT_TILES):
+                nc.vector.tensor_tensor(
+                    out=step[:, j, :], in0=update[i][:, j, :], in1=diff[:, j, :], op=ALU.mult
+                )
             turned = psum.tile([P, ROW_TILES, UNIT], F32, tag="out_turned", bufs=2)
             for r in range(ROW_TILES):
                 for j in range(UNIT_TILES):

@@ -27,7 +27,7 @@ UNITS = BLOCKS * BLOCK // UNIT
 UNITS_PER_BLOCK = BLOCK // UNIT
 BIAS_TILES = BLOCKS * GATES * BLOCK // P
 RUN = 4
-CAND_COLUMNS_ON_SCALAR = 96
+CAND_COLUMNS_ON_SCALAR = 192
 GPSIMD_COLUMNS = 128
 
 FLOPS = 2 * ROWS * BLOCKS * BLOCK * GATES * BLOCK
@@ -126,25 +126,16 @@ def tile_blockrecurrentmodel_pb_kernel(tc, h, d, W_gate, b_gate, out):
                 first = gate * BLOCK + part * UNIT
                 piece = w_tiles[g][:, :, first : first + UNIT]
                 place = grouped[:, gate * UNIT : (gate + 1) * UNIT, :]
+                src = piece.rearrange("p t (c s) -> p c t s", s=RUN)
+                dst = place.rearrange("p (c s) t -> p c t s", s=RUN)
                 if gate == RESET:
-                    for lo in range(0, UNIT, GPSIMD_COLUMNS):
-                        nc.gpsimd.tensor_scalar(
-                            out=place[:, lo : lo + GPSIMD_COLUMNS, :],
-                            in0=piece[:, :, lo : lo + GPSIMD_COLUMNS].rearrange("p t w -> p w t"),
-                            scalar1=1.0,
-                            scalar2=0.0,
-                            op0=ALU.mult,
-                            op1=ALU.add,
-                        )
+                    nc.vector.tensor_copy(out=dst, in_=src)
+                elif gate == UPDATE:
+                    nc.scalar.copy(out=dst, in_=src)
                 else:
-                    src = piece.rearrange("p t (c s) -> p c t s", s=RUN)
-                    dst = place.rearrange("p (c s) t -> p c t s", s=RUN)
-                    if gate == UPDATE:
-                        nc.scalar.copy(out=dst, in_=src)
-                    else:
-                        cut = CAND_COLUMNS_ON_SCALAR // RUN
-                        nc.scalar.copy(out=dst[:, :cut], in_=src[:, :cut])
-                        nc.vector.tensor_copy(out=dst[:, cut:], in_=src[:, cut:])
+                    cut = CAND_COLUMNS_ON_SCALAR // RUN
+                    nc.scalar.copy(out=dst[:, :cut], in_=src[:, :cut])
+                    nc.vector.tensor_copy(out=dst[:, cut:], in_=src[:, cut:])
             w_grouped[i] = grouped
 
         def quantise_weights(i):
@@ -240,7 +231,7 @@ def tile_blockrecurrentmodel_pb_kernel(tc, h, d, W_gate, b_gate, out):
 
         def add_d_and_store(i):
             g, part = divmod(i, UNITS_PER_BLOCK)
-            result = work.tile([P, ROW_TILES, UNIT], F32, tag="result", bufs=3)
+            result = work.tile([P, ROW_TILES, UNIT], F32, tag="result", bufs=8)
             nc.vector.tensor_tensor(
                 out=result[:],
                 in0=out_turned[i][:],

@@ -26,9 +26,8 @@ UNIT_TILES = UNIT // P
 UNITS = BLOCKS * BLOCK // UNIT
 UNITS_PER_BLOCK = BLOCK // UNIT
 BIAS_TILES = BLOCKS * GATES * BLOCK // P
+SUBTRACTED = [i for i in range(12) if i % 3 != 0]
 RUN = 4
-CAND_COLUMNS_ON_SCALAR = 192
-GPSIMD_COLUMNS = 128
 
 FLOPS = 2 * ROWS * BLOCKS * BLOCK * GATES * BLOCK
 
@@ -55,21 +54,31 @@ def tile_blockrecurrentmodel_pb_kernel(tc, h, d, W_gate, b_gate, out):
         h_tiles, w_tiles, d_tiles = [], [], []
         for g in range(BLOCKS):
             h_sb = inputs.tile([P, ROW_TILES, BLOCK], BF16)
-            nc.sync.dma_start(out=h_sb[:], in_=h_view[g])
-            w_sb = inputs.tile([P, PACK, GATES * BLOCK], BF16)
-            pieces = GATES if g == 0 else 1
-            width = GATES * BLOCK // pieces
-            for s in range(pieces):
-                cols = slice(s * width, (s + 1) * width)
-                nc.sync.dma_start(out=w_sb[:, :, cols], in_=w_view[g][:, :, cols])
+            if g == 0:
+                w_pieces = []
+                for gate in range(GATES):
+                    if gate == GATES - 1:
+                        nc.sync.dma_start(out=h_sb[:], in_=h_view[g])
+                    piece = const.tile([P, PACK, BLOCK], BF16, tag="first_weights_%d" % gate)
+                    nc.sync.dma_start(out=piece[:], in_=w_view[g][:, :, gate * BLOCK : (gate + 1) * BLOCK])
+                    w_pieces.append(piece[:])
+            else:
+                nc.sync.dma_start(out=h_sb[:], in_=h_view[g])
+                w_sb = inputs.tile([P, PACK, GATES * BLOCK], BF16, bufs=BLOCKS - 1)
+                nc.sync.dma_start(out=w_sb[:], in_=w_view[g])
+                w_pieces = [w_sb[:, :, gate * BLOCK : (gate + 1) * BLOCK] for gate in range(GATES)]
             d_sb = inputs.tile([P, ROW_TILES, BLOCK], BF16)
             nc.sync.dma_start(out=d_sb[:], in_=d_view[g])
             h_tiles.append(h_sb)
-            w_tiles.append(w_sb)
+            w_tiles.append(w_pieces)
             d_tiles.append(d_sb)
 
         ident_f32 = const.tile([P, P], F32)
         make_identity(nc, ident_f32[:])
+        negative_ident = const.tile([P, P], F32)
+        nc.gpsimd.tensor_scalar(
+            out=negative_ident[:], in0=ident_f32[:], scalar1=-1.0, scalar2=0.0, op0=ALU.mult, op1=ALU.add
+        )
         ident_bf16 = const.tile([P, P], BF16)
         make_identity(nc, ident_bf16[:])
 
@@ -79,12 +88,14 @@ def tile_blockrecurrentmodel_pb_kernel(tc, h, d, W_gate, b_gate, out):
         nc.scalar.activation(out=warm[:], in_=zero[:], func=ACT.Sigmoid)
 
         nc.vector.memset(bias_rows[BIAS_TILES:P, :], 0.0)
-        bias_turned = psum.tile([P, P], BF16, tag="h_turned")
+        bias_turned = psum.tile([P, P], BF16, tag="out_turned", bufs=2)
         nc.tensor.transpose(bias_turned[:], bias_rows[:], ident_bf16[:])
         bias = const.tile([P, BIAS_TILES], F32)
         nc.vector.tensor_copy(out=bias[:], in_=bias_turned[:, 0:BIAS_TILES])
         update_bias = bias[:].rearrange("p (g a q) -> p g a q", g=BLOCKS, a=GATES)[:, :, UPDATE, :]
-        nc.vector.tensor_scalar_add(out=update_bias, in0=update_bias, scalar1=-1.0)
+        nc.vector.tensor_scalar(
+            out=update_bias, in0=update_bias, scalar1=-1.0, scalar2=1.0, op0=ALU.mult, op1=ALU.add
+        )
 
         def bias_column(i, gate, j):
             g, part = divmod(i, UNITS_PER_BLOCK)
@@ -92,7 +103,7 @@ def tile_blockrecurrentmodel_pb_kernel(tc, h, d, W_gate, b_gate, out):
             return bias[:, col : col + 1]
 
         h_turned, h_grouped, h_codes, h_scales = {}, {}, {}, {}
-        w_grouped, w_codes, w_scales = {}, {}, {}
+        w_grouped, w_quantised = {}, {}
         gates, d_turned, out_turned = {}, {}, {}
         reset, update, gated, cand = {}, {}, {}, {}
 
@@ -119,48 +130,49 @@ def tile_blockrecurrentmodel_pb_kernel(tc, h, d, W_gate, b_gate, out):
             nc.vector.quantize_mx(out=codes[:].bitcast(FP8X4), scales=scales[:], in_=h_grouped[g][:])
             h_codes[g], h_scales[g] = codes, scales
 
-        def regroup_weights(i):
-            g, part = divmod(i, UNITS_PER_BLOCK)
-            grouped = stage.tile([P, GATES * UNIT, PACK], BF16, align_bytes=64, tag="w_grouped")
-            for gate in range(GATES):
-                first = gate * BLOCK + part * UNIT
-                piece = w_tiles[g][:, :, first : first + UNIT]
-                place = grouped[:, gate * UNIT : (gate + 1) * UNIT, :]
-                src = piece.rearrange("p t (c s) -> p c t s", s=RUN)
-                dst = place.rearrange("p (c s) t -> p c t s", s=RUN)
-                if gate == RESET:
-                    nc.vector.tensor_copy(out=dst, in_=src)
-                elif gate == UPDATE:
-                    nc.scalar.copy(out=dst, in_=src)
-                else:
-                    cut = CAND_COLUMNS_ON_SCALAR // RUN
-                    nc.scalar.copy(out=dst[:, :cut], in_=src[:, :cut])
-                    nc.vector.tensor_copy(out=dst[:, cut:], in_=src[:, cut:])
-            w_grouped[i] = grouped
+        def regroup_weights(chunk):
+            first_unit, units = chunk
+            g, part = divmod(first_unit, UNITS_PER_BLOCK)
+            width = units * UNIT
+            grouped = stage.tile([P, GATES * width, PACK], BF16, align_bytes=64, tag="w_grouped")
+            for gate, lo, hi, copy in (
+                (RESET, 0, width, nc.vector.tensor_copy),
+                (UPDATE, 0, width, nc.scalar.copy),
+                (CAND, 0, width, nc.vector.tensor_copy),
+            ):
+                first = part * UNIT
+                src = w_tiles[g][gate][:, :, first + lo : first + hi].rearrange("p t (c s) -> p c t s", s=RUN)
+                place = grouped[:, gate * width + lo : gate * width + hi, :]
+                copy(out=place.rearrange("p (c s) t -> p c t s", s=RUN), in_=src)
+            w_grouped[first_unit] = grouped
 
-        def quantise_weights(i):
-            codes = quant.tile([P, GATES * UNIT], U32, align_bytes=64, tag="w_codes")
-            scales = quant.tile([P, GATES * UNIT], U8, align_bytes=64, tag="w_scales")
-            flat = w_grouped[i][:].rearrange("p w t -> p (w t)")
-            for lo, hi in ((0, 2 * UNIT), (2 * UNIT, 3 * UNIT)):
+        def quantise_weights(chunk):
+            first_unit, units = chunk
+            width = units * UNIT
+            codes = quant.tile([P, GATES * width], U32, align_bytes=64, tag="w_codes")
+            scales = quant.tile([P, GATES * width], U8, align_bytes=64, tag="w_scales")
+            flat = w_grouped[first_unit][:].rearrange("p w t -> p (w t)")
+            for lo, hi in ((0, 2 * width), (2 * width, 3 * width)):
                 nc.vector.quantize_mx(
                     out=codes[:, lo:hi].bitcast(FP8X4),
                     scales=scales[:, lo:hi],
                     in_=flat[:, lo * PACK : hi * PACK],
                 )
-            w_codes[i], w_scales[i] = codes, scales
+            for k in range(units):
+                w_quantised[first_unit + k] = (codes, scales, width, k * UNIT)
 
         def multiply(i):
             g = i // UNITS_PER_BLOCK
+            codes, scales, width, offset = w_quantised[i]
             banks = []
             for gate, tag in ((RESET, "r"), (UPDATE, "u"), (CAND, "c")):
                 bank = psum.tile([P, UNIT_TILES, ROWS], F32, tag=tag)
                 for j in range(UNIT_TILES):
-                    cols = slice(gate * UNIT + j * P, gate * UNIT + (j + 1) * P)
+                    first = gate * width + offset + j * P
                     nc.tensor.matmul_mx(
                         out=bank[:, j, :],
-                        lhsT=w_codes[i][:, cols].bitcast(FP8X4),
-                        lhsT_scale=w_scales[i][:, cols],
+                        lhsT=codes[:, first : first + P].bitcast(FP8X4),
+                        lhsT_scale=scales[:, first : first + P],
                         rhs=h_codes[g][:].bitcast(FP8X4),
                         rhs_scale=h_scales[g][:],
                         start=True,
@@ -184,10 +196,14 @@ def tile_blockrecurrentmodel_pb_kernel(tc, h, d, W_gate, b_gate, out):
             r_bank, u_bank, c_bank = gates[i]
             reset_sb = work.tile([P, UNIT_TILES, ROWS], F32, tag="reset")
             update_sb = work.tile([P, UNIT_TILES, ROWS], F32, tag="update")
-            for gate, bank, act in ((RESET, r_bank, reset_sb), (UPDATE, u_bank, update_sb)):
+            for gate, bank, act, scale in ((RESET, r_bank, reset_sb, 1.0), (UPDATE, u_bank, update_sb, -1.0)):
                 for j in range(UNIT_TILES):
                     nc.scalar.activation(
-                        out=act[:, j, :], in_=bank[:, j, :], func=ACT.Sigmoid, bias=bias_column(i, gate, j)
+                        out=act[:, j, :],
+                        in_=bank[:, j, :],
+                        func=ACT.Sigmoid,
+                        bias=bias_column(i, gate, j),
+                        scale=scale,
                     )
             reset[i], update[i] = reset_sb, update_sb
 
@@ -207,47 +223,78 @@ def tile_blockrecurrentmodel_pb_kernel(tc, h, d, W_gate, b_gate, out):
 
         def candidate(i):
             cand_sb = work.tile([P, UNIT_TILES, ROWS], F32, tag="cand")
-            nc.scalar.activation(out=cand_sb[:], in_=gated[i][:], func=ACT.Tanh)
+            nc.scalar.activation(
+                out=cand_sb[:], in_=gated[i][:], func=ACT.Tanh, scale=1.0 if i in SUBTRACTED else -1.0
+            )
             cand[i] = cand_sb
 
         def blend(i):
-            diff = work.tile([P, UNIT_TILES, ROWS], F32, tag="diff")
             step = work.tile([P, UNIT_TILES, ROWS], F32, tag="step")
-            for j in range(UNIT_TILES):
-                nc.vector.tensor_tensor(
-                    out=diff[:, j, :], in0=cand[i][:, j, :], in1=d_turned[i][:, j, :], op=ALU.subtract
-                )
-            for j in range(UNIT_TILES):
-                nc.vector.tensor_tensor(
-                    out=step[:, j, :], in0=update[i][:, j, :], in1=diff[:, j, :], op=ALU.mult
-                )
-            turned = psum.tile([P, ROW_TILES, UNIT], F32, tag="out_turned", bufs=2)
-            for r in range(ROW_TILES):
+            if i in SUBTRACTED:
+                g, part = divmod(i, UNITS_PER_BLOCK)
+                difference = psum.tile([P, UNIT_TILES, ROWS], F32, tag="d_turned", bufs=2)
                 for j in range(UNIT_TILES):
-                    nc.tensor.transpose(
-                        turned[:, r, j * P : (j + 1) * P], step[:, j, r * P : (r + 1) * P], ident_f32[:]
-                    )
+                    lo = part * UNIT + j * P
+                    for r in range(ROW_TILES):
+                        nc.tensor.matmul(
+                            out=difference[:, j, r * P : (r + 1) * P],
+                            lhsT=d_tiles[g][:, r, lo : lo + P],
+                            rhs=ident_bf16[:],
+                            start=(j == 0 and r == 0),
+                            stop=False,
+                        )
+                nc.tensor.matmul(
+                    out=difference[:], lhsT=negative_ident[:], rhs=cand[i][:], start=False, stop=True
+                )
+                nc.vector.tensor_tensor(out=step[:], in0=update[i][:], in1=difference[:], op=ALU.mult)
+                kept = cand[i]
+            else:
+                kept = work.tile([P, UNIT_TILES, ROWS], F32, tag="kept")
+                nc.vector.tensor_tensor(out=kept[:], in0=update[i][:], in1=d_turned[i][:], op=ALU.mult)
+                nc.vector.scalar_tensor_tensor(
+                    out=step[:], in0=update[i][:], scalar=-1.0, in1=cand[i][:], op0=ALU.add, op1=ALU.mult
+                )
+            groups = ((0,), (1,)) if i == UNITS - 1 else ((0, 1),)
+            turned = {}
+            for rows in groups:
+                bank = psum.tile([P, len(rows), UNIT], F32, tag="out_turned", bufs=2)
+                turned[rows] = bank
+            for term in (kept, step):
+                for rows in groups:
+                    for r in rows:
+                        for j in range(UNIT_TILES):
+                            nc.tensor.matmul(
+                                out=turned[rows][:, r - rows[0], j * P : (j + 1) * P],
+                                lhsT=term[:, j, r * P : (r + 1) * P],
+                                rhs=ident_f32[:],
+                                is_transpose=True,
+                                start=(term is kept and r == rows[0] and j == 0),
+                                stop=(term is step and r == rows[-1] and j == UNIT_TILES - 1),
+                            )
             out_turned[i] = turned
 
         def add_d_and_store(i):
-            g, part = divmod(i, UNITS_PER_BLOCK)
-            result = work.tile([P, ROW_TILES, UNIT], F32, tag="result", bufs=8)
-            nc.vector.tensor_tensor(
-                out=result[:],
-                in0=out_turned[i][:],
-                in1=d_tiles[g][:, :, part * UNIT : (part + 1) * UNIT],
-                op=ALU.add,
-            )
-            nc.sync.dma_start(out=out_view[i], in_=result[:])
+            for rows, bank in out_turned[i].items():
+                result = work.tile([P, len(rows), UNIT], F32, tag="result", bufs=6)
+                copy = nc.vector.tensor_copy if rows == (1,) else nc.scalar.copy
+                copy(out=result[:], in_=bank[:])
+                nc.sync.dma_start(out=out_view[i][:, rows[0] : rows[-1] + 1, :], in_=result[:])
 
         def exists(i):
             return 0 <= i < UNITS
 
+        chunks = {}
+        for g in range(BLOCKS):
+            units = 1 if g in (0, BLOCKS - 1) else UNITS_PER_BLOCK
+            for i in range(g * UNITS_PER_BLOCK, (g + 1) * UNITS_PER_BLOCK, units):
+                chunks[i] = (i, units)
+
         for t in range(-3, UNITS + 1):
             if exists(t + 1):
                 sigmoids(t + 1)
+            if t + 2 in chunks:
+                quantise_weights(chunks[t + 2])
             if exists(t + 2):
-                quantise_weights(t + 2)
                 if (t + 2) % UNITS_PER_BLOCK == 0:
                     quantise_h((t + 2) // UNITS_PER_BLOCK)
             if exists(t + 1):
@@ -256,7 +303,7 @@ def tile_blockrecurrentmodel_pb_kernel(tc, h, d, W_gate, b_gate, out):
                 multiply(t + 2)
             if exists(t + 3) and (t + 3) % UNITS_PER_BLOCK == 0:
                 turn_h((t + 3) // UNITS_PER_BLOCK)
-            if exists(t + 1):
+            if exists(t + 1) and t + 1 not in SUBTRACTED:
                 turn_d(t + 1)
             if exists(t):
                 candidate(t)
@@ -267,4 +314,5 @@ def tile_blockrecurrentmodel_pb_kernel(tc, h, d, W_gate, b_gate, out):
             if exists(t + 3):
                 if (t + 3) % UNITS_PER_BLOCK == 0:
                     group_h((t + 3) // UNITS_PER_BLOCK)
-                regroup_weights(t + 3)
+                if t + 3 in chunks:
+                    regroup_weights(chunks[t + 3])

@@ -26,7 +26,9 @@ UNIT_TILES = UNIT // P
 UNITS = BLOCKS * BLOCK // UNIT
 UNITS_PER_BLOCK = BLOCK // UNIT
 BIAS_TILES = BLOCKS * GATES * BLOCK // P
-SUBTRACTED = [i for i in range(12) if i % 3 != 0]
+SUBTRACTED = [1, 3, 5, 7, 9, 11]
+VECTOR_OUT = (14,)
+W_BUFS = 7
 RUN = 4
 
 FLOPS = 2 * ROWS * BLOCKS * BLOCK * GATES * BLOCK
@@ -50,29 +52,43 @@ def tile_blockrecurrentmodel_pb_kernel(tc, h, d, W_gate, b_gate, out):
         psum = ctx.enter_context(tc.psum_pool(name="psum", bufs=1))
 
         bias_rows = const.tile([P, P], BF16)
-        nc.scalar.dma_start(out=bias_rows[0:BIAS_TILES, :], in_=bias_view)
-        h_tiles, w_tiles, d_tiles = [], [], []
-        for g in range(BLOCKS):
-            h_sb = inputs.tile([P, ROW_TILES, BLOCK], BF16)
-            if g == 0:
-                w_pieces = []
-                for gate in range(GATES):
-                    if gate == GATES - 1:
-                        nc.sync.dma_start(out=h_sb[:], in_=h_view[g])
-                    piece = const.tile([P, PACK, BLOCK], BF16, tag="first_weights_%d" % gate)
-                    nc.sync.dma_start(out=piece[:], in_=w_view[g][:, :, gate * BLOCK : (gate + 1) * BLOCK])
-                    w_pieces.append(piece[:])
-            else:
-                nc.sync.dma_start(out=h_sb[:], in_=h_view[g])
-                w_sb = inputs.tile([P, PACK, GATES * BLOCK], BF16, bufs=BLOCKS - 1)
-                nc.sync.dma_start(out=w_sb[:], in_=w_view[g])
-                w_pieces = [w_sb[:, :, gate * BLOCK : (gate + 1) * BLOCK] for gate in range(GATES)]
-            d_sb = inputs.tile([P, ROW_TILES, BLOCK], BF16)
-            nc.sync.dma_start(out=d_sb[:], in_=d_view[g])
-            h_tiles.append(h_sb)
-            w_tiles.append(w_pieces)
-            d_tiles.append(d_sb)
+        h_tiles, w_tiles, d_tiles = {}, {}, {}
 
+        def load_bias():
+            nc.sync.dma_start(out=bias_rows[0:BIAS_TILES, :], in_=bias_view)
+
+        def load_h(g):
+            h_sb = inputs.tile([P, ROW_TILES, BLOCK], BF16, tag="h_sb")
+            nc.sync.dma_start(out=h_sb[:], in_=h_view[g])
+            h_tiles[g] = h_sb
+
+        def load_d(g):
+            d_sb = inputs.tile([P, ROW_TILES, BLOCK], BF16, tag="d_sb")
+            nc.sync.dma_start(out=d_sb[:], in_=d_view[g])
+            d_tiles[g] = d_sb
+
+        def load_w(g, lo=0, hi=GATES):
+            if lo == 0 and hi == GATES:
+                piece = inputs.tile([P, PACK, GATES * BLOCK], BF16, tag="w_sb", bufs=W_BUFS)
+                nc.sync.dma_start(out=piece[:], in_=w_view[g])
+            else:
+                piece = const.tile([P, PACK, (hi - lo) * BLOCK], BF16, tag="w_%d_%d" % (g, lo))
+                nc.sync.dma_start(out=piece[:], in_=w_view[g][:, :, lo * BLOCK : hi * BLOCK])
+            for gate in range(lo, hi):
+                w_tiles[g, gate] = piece[:, :, (gate - lo) * BLOCK : (gate - lo + 1) * BLOCK]
+
+        load_h(0)
+        load_w(0, 0, 1)
+        load_bias()
+        load_w(0, 1, 3)
+        load_h(1)
+        load_w(1)
+        load_d(0)
+        for g in range(2, BLOCKS):
+            load_h(g)
+            load_w(g)
+            load_d(g - 1)
+        load_d(BLOCKS - 1)
         ident_f32 = const.tile([P, P], F32)
         make_identity(nc, ident_f32[:])
         negative_ident = const.tile([P, P], F32)
@@ -88,14 +104,16 @@ def tile_blockrecurrentmodel_pb_kernel(tc, h, d, W_gate, b_gate, out):
         nc.scalar.activation(out=warm[:], in_=zero[:], func=ACT.Sigmoid)
 
         nc.vector.memset(bias_rows[BIAS_TILES:P, :], 0.0)
-        bias_turned = psum.tile([P, P], BF16, tag="out_turned", bufs=2)
-        nc.tensor.transpose(bias_turned[:], bias_rows[:], ident_bf16[:])
         bias = const.tile([P, BIAS_TILES], F32)
-        nc.vector.tensor_copy(out=bias[:], in_=bias_turned[:, 0:BIAS_TILES])
-        update_bias = bias[:].rearrange("p (g a q) -> p g a q", g=BLOCKS, a=GATES)[:, :, UPDATE, :]
-        nc.vector.tensor_scalar(
-            out=update_bias, in0=update_bias, scalar1=-1.0, scalar2=1.0, op0=ALU.mult, op1=ALU.add
-        )
+
+        def turn_bias():
+            bias_turned = psum.tile([P, P], BF16, tag="out_turned", bufs=2)
+            nc.tensor.transpose(bias_turned[:], bias_rows[:], ident_bf16[:])
+            nc.vector.tensor_copy(out=bias[:], in_=bias_turned[:, 0:BIAS_TILES])
+            update_bias = bias[:].rearrange("p (g a q) -> p g a q", g=BLOCKS, a=GATES)[:, :, UPDATE, :]
+            nc.vector.tensor_scalar(
+                out=update_bias, in0=update_bias, scalar1=-1.0, scalar2=1.0, op0=ALU.mult, op1=ALU.add
+            )
 
         def bias_column(i, gate, j):
             g, part = divmod(i, UNITS_PER_BLOCK)
@@ -106,6 +124,7 @@ def tile_blockrecurrentmodel_pb_kernel(tc, h, d, W_gate, b_gate, out):
         w_grouped, w_quantised = {}, {}
         gates, d_turned, out_turned = {}, {}, {}
         reset, update, gated, cand = {}, {}, {}, {}
+        kept_of, step_of = {}, {}
 
         def turn_h(g):
             words = h_tiles[g][:].rearrange("p r f -> p (r f)").bitcast(F32)
@@ -115,6 +134,9 @@ def tile_blockrecurrentmodel_pb_kernel(tc, h, d, W_gate, b_gate, out):
                 for r in range(ROW_TILES):
                     nc.tensor.transpose(turned[:, u, r * P : (r + 1) * P], words[:, r, u, :], ident_f32[:])
             h_turned[g] = turned
+
+        def by_gpsimd(out, in_):
+            nc.gpsimd.tensor_scalar(out=out, in0=in_, scalar1=1.0, scalar2=0.0, op0=ALU.mult, op1=ALU.add)
 
         def group_h(g):
             grouped = stage.tile([P, ROWS * PACK], BF16, align_bytes=64, tag="h_grouped")
@@ -130,56 +152,66 @@ def tile_blockrecurrentmodel_pb_kernel(tc, h, d, W_gate, b_gate, out):
             nc.vector.quantize_mx(out=codes[:].bitcast(FP8X4), scales=scales[:], in_=h_grouped[g][:])
             h_codes[g], h_scales[g] = codes, scales
 
-        def regroup_weights(chunk):
-            first_unit, units = chunk
+        def new_grouped(first_unit):
+            width = chunk_units[first_unit] * UNIT
+            main = stage.tile([P, 2 * width, PACK], BF16, align_bytes=64, tag="w_grouped", bufs=2)
+            w_grouped[first_unit, RESET] = main[:, 0:width, :]
+            w_grouped[first_unit, CAND] = main[:, width : 2 * width, :]
+            w_grouped[first_unit] = main
+
+        def new_update(first_unit):
+            width = chunk_units[first_unit] * UNIT
+            tile = stage.tile([P, width, PACK], BF16, align_bytes=64, tag="u_grouped_%d" % chunk_units[first_unit], bufs=1 if chunk_units[first_unit] > 1 else 2)
+            w_grouped[first_unit, UPDATE] = tile[:]
+
+        def regroup(first_unit, gate, copy, lo=0, hi=None, run=RUN):
+            if (first_unit, gate) not in w_grouped:
+                if gate == UPDATE:
+                    new_update(first_unit)
+                else:
+                    new_grouped(first_unit)
+            place = w_grouped[first_unit, gate]
             g, part = divmod(first_unit, UNITS_PER_BLOCK)
-            width = units * UNIT
-            grouped = stage.tile([P, GATES * width, PACK], BF16, align_bytes=64, tag="w_grouped")
-            for gate, lo, hi, copy in (
-                (RESET, 0, width, nc.vector.tensor_copy),
-                (UPDATE, 0, width, nc.scalar.copy),
-                (CAND, 0, width, nc.vector.tensor_copy),
-            ):
-                first = part * UNIT
-                src = w_tiles[g][gate][:, :, first + lo : first + hi].rearrange("p t (c s) -> p c t s", s=RUN)
-                place = grouped[:, gate * width + lo : gate * width + hi, :]
-                copy(out=place.rearrange("p (c s) t -> p c t s", s=RUN), in_=src)
-            w_grouped[first_unit] = grouped
+            first = part * UNIT
+            hi = place.shape[1] if hi is None else hi
+            src = w_tiles[g, gate][:, :, first + lo : first + hi]
+            place = place[:, lo:hi, :]
+            if run == 1:
+                copy(out=place, in_=src.rearrange("p t c -> p c t"))
+            else:
+                copy(out=place.rearrange("p (c s) t -> p c t s", s=run), in_=src.rearrange("p t (c s) -> p c t s", s=run))
 
-        def quantise_weights(chunk):
-            first_unit, units = chunk
-            width = units * UNIT
-            codes = quant.tile([P, GATES * width], U32, align_bytes=64, tag="w_codes")
-            scales = quant.tile([P, GATES * width], U8, align_bytes=64, tag="w_scales")
-            flat = w_grouped[first_unit][:].rearrange("p w t -> p (w t)")
-            for lo, hi in ((0, 2 * width), (2 * width, 3 * width)):
-                nc.vector.quantize_mx(
-                    out=codes[:, lo:hi].bitcast(FP8X4),
-                    scales=scales[:, lo:hi],
-                    in_=flat[:, lo * PACK : hi * PACK],
-                )
-            for k in range(units):
-                w_quantised[first_unit + k] = (codes, scales, width, k * UNIT)
+        def quantise(first_unit, gates_in):
+            width = chunk_units[first_unit] * UNIT
+            n = len(gates_in) * width
+            name = "".join("ruc"[gate] for gate in gates_in) + "_%d" % chunk_units[first_unit]
+            codes = quant.tile([P, n], U32, align_bytes=64, tag="codes_" + name, bufs=2)
+            scales = quant.tile([P, n], U8, align_bytes=64, tag="scales_" + name, bufs=2)
+            src = w_grouped[first_unit][:] if len(gates_in) == 2 else w_grouped[first_unit, gates_in[0]]
+            nc.vector.quantize_mx(
+                out=codes[:].bitcast(FP8X4), scales=scales[:], in_=src.rearrange("p w t -> p (w t)")
+            )
+            for k, gate in enumerate(gates_in):
+                for unit in range(chunk_units[first_unit]):
+                    w_quantised[first_unit + unit, gate] = (codes, scales, k * width + unit * UNIT)
 
-        def multiply(i):
+        def multiply(i, gates_in=(RESET, UPDATE, CAND)):
             g = i // UNITS_PER_BLOCK
-            codes, scales, width, offset = w_quantised[i]
-            banks = []
-            for gate, tag in ((RESET, "r"), (UPDATE, "u"), (CAND, "c")):
-                bank = psum.tile([P, UNIT_TILES, ROWS], F32, tag=tag)
+            for gate in gates_in:
+                codes, scales, first = w_quantised[i, gate]
+                bank = psum.tile([P, UNIT_TILES, ROWS], F32, tag="ruc"[gate])
                 for j in range(UNIT_TILES):
-                    first = gate * width + offset + j * P
+                    lo = first + j * P
                     nc.tensor.matmul_mx(
                         out=bank[:, j, :],
-                        lhsT=codes[:, first : first + P].bitcast(FP8X4),
-                        lhsT_scale=scales[:, first : first + P],
+                        lhsT=codes[:, lo : lo + P].bitcast(FP8X4),
+                        lhsT_scale=scales[:, lo : lo + P],
                         rhs=h_codes[g][:].bitcast(FP8X4),
                         rhs_scale=h_scales[g][:],
                         start=True,
                         stop=True,
                     )
-                banks.append(bank)
-            gates[i] = banks
+                gates[i, gate] = bank
 
         def turn_d(i):
             g, part = divmod(i, UNITS_PER_BLOCK)
@@ -192,23 +224,24 @@ def tile_blockrecurrentmodel_pb_kernel(tc, h, d, W_gate, b_gate, out):
                     )
             d_turned[i] = turned
 
-        def sigmoids(i):
-            r_bank, u_bank, c_bank = gates[i]
-            reset_sb = work.tile([P, UNIT_TILES, ROWS], F32, tag="reset")
-            update_sb = work.tile([P, UNIT_TILES, ROWS], F32, tag="update")
-            for gate, bank, act, scale in ((RESET, r_bank, reset_sb, 1.0), (UPDATE, u_bank, update_sb, -1.0)):
-                for j in range(UNIT_TILES):
-                    nc.scalar.activation(
-                        out=act[:, j, :],
-                        in_=bank[:, j, :],
-                        func=ACT.Sigmoid,
-                        bias=bias_column(i, gate, j),
-                        scale=scale,
-                    )
-            reset[i], update[i] = reset_sb, update_sb
+        def sigmoid(i, gate):
+            if gate == RESET:
+                act = work.tile([P, UNIT_TILES, ROWS], F32, tag="reset", bufs=3)
+                reset[i] = act
+            else:
+                act = work.tile([P, UNIT_TILES, ROWS], F32, tag="update", bufs=4)
+                update[i] = act
+            for j in range(UNIT_TILES):
+                nc.scalar.activation(
+                    out=act[:, j, :],
+                    in_=gates[i, gate][:, j, :],
+                    func=ACT.Sigmoid,
+                    bias=bias_column(i, gate, j),
+                    scale=1.0 if gate == RESET else -1.0,
+                )
 
         def gate_candidate(i):
-            r_bank, u_bank, c_bank = gates[i]
+            c_bank = gates[i, CAND]
             gated_sb = work.tile([P, UNIT_TILES, ROWS], F32, tag="gated")
             for j in range(UNIT_TILES):
                 nc.vector.scalar_tensor_tensor(
@@ -222,44 +255,61 @@ def tile_blockrecurrentmodel_pb_kernel(tc, h, d, W_gate, b_gate, out):
             gated[i] = gated_sb
 
         def candidate(i):
-            cand_sb = work.tile([P, UNIT_TILES, ROWS], F32, tag="cand")
+            cand_sb = work.tile([P, UNIT_TILES, ROWS], F32, tag="cand", bufs=3)
             nc.scalar.activation(
                 out=cand_sb[:], in_=gated[i][:], func=ACT.Tanh, scale=1.0 if i in SUBTRACTED else -1.0
             )
             cand[i] = cand_sb
 
-        def blend(i):
-            step = work.tile([P, UNIT_TILES, ROWS], F32, tag="step")
+        def open_d(i):
+            if i not in SUBTRACTED:
+                turn_d(i)
+                return
+            g, part = divmod(i, UNITS_PER_BLOCK)
+            difference = psum.tile([P, UNIT_TILES, ROWS], F32, tag="d_turned", bufs=2)
+            for j in range(UNIT_TILES):
+                lo = part * UNIT + j * P
+                for r in range(ROW_TILES):
+                    nc.tensor.matmul(
+                        out=difference[:, j, r * P : (r + 1) * P],
+                        lhsT=d_tiles[g][:, r, lo : lo + P],
+                        rhs=ident_bf16[:],
+                        start=(j == 0 and r == 0),
+                        stop=False,
+                    )
+            d_turned[i] = difference
+
+        def subtract(i):
             if i in SUBTRACTED:
-                g, part = divmod(i, UNITS_PER_BLOCK)
-                difference = psum.tile([P, UNIT_TILES, ROWS], F32, tag="d_turned", bufs=2)
-                for j in range(UNIT_TILES):
-                    lo = part * UNIT + j * P
-                    for r in range(ROW_TILES):
-                        nc.tensor.matmul(
-                            out=difference[:, j, r * P : (r + 1) * P],
-                            lhsT=d_tiles[g][:, r, lo : lo + P],
-                            rhs=ident_bf16[:],
-                            start=(j == 0 and r == 0),
-                            stop=False,
-                        )
                 nc.tensor.matmul(
-                    out=difference[:], lhsT=negative_ident[:], rhs=cand[i][:], start=False, stop=True
+                    out=d_turned[i][:], lhsT=negative_ident[:], rhs=cand[i][:], start=False, stop=True
                 )
-                nc.vector.tensor_tensor(out=step[:], in0=update[i][:], in1=difference[:], op=ALU.mult)
-                kept = cand[i]
+
+        def keep_d(i):
+            if i in SUBTRACTED:
+                kept_of[i] = cand[i]
             else:
                 kept = work.tile([P, UNIT_TILES, ROWS], F32, tag="kept")
                 nc.vector.tensor_tensor(out=kept[:], in0=update[i][:], in1=d_turned[i][:], op=ALU.mult)
+                kept_of[i] = kept
+
+        def blend(i):
+            step = work.tile([P, UNIT_TILES, ROWS], F32, tag="step")
+            if i in SUBTRACTED:
+                nc.vector.tensor_tensor(out=step[:], in0=update[i][:], in1=d_turned[i][:], op=ALU.mult)
+            else:
                 nc.vector.scalar_tensor_tensor(
                     out=step[:], in0=update[i][:], scalar=-1.0, in1=cand[i][:], op0=ALU.add, op1=ALU.mult
                 )
+            step_of[i] = step
+
+        def back(i):
             groups = ((0,), (1,)) if i == UNITS - 1 else ((0, 1),)
             turned = {}
             for rows in groups:
                 bank = psum.tile([P, len(rows), UNIT], F32, tag="out_turned", bufs=2)
                 turned[rows] = bank
-            for term in (kept, step):
+            for term in (kept_of[i], step_of[i]):
                 for rows in groups:
                     for r in rows:
                         for j in range(UNIT_TILES):
@@ -268,51 +318,175 @@ def tile_blockrecurrentmodel_pb_kernel(tc, h, d, W_gate, b_gate, out):
                                 lhsT=term[:, j, r * P : (r + 1) * P],
                                 rhs=ident_f32[:],
                                 is_transpose=True,
-                                start=(term is kept and r == rows[0] and j == 0),
-                                stop=(term is step and r == rows[-1] and j == UNIT_TILES - 1),
+                                start=(term is kept_of[i] and r == rows[0] and j == 0),
+                                stop=(term is step_of[i] and r == rows[-1] and j == UNIT_TILES - 1),
                             )
             out_turned[i] = turned
+
+        def back_out(i):
+            if 0 <= i < UNITS:
+                add_d_and_store(i)
 
         def add_d_and_store(i):
             for rows, bank in out_turned[i].items():
                 result = work.tile([P, len(rows), UNIT], F32, tag="result", bufs=6)
-                copy = nc.vector.tensor_copy if rows == (1,) else nc.scalar.copy
+                copy = nc.vector.tensor_copy if rows == (1,) or i in VECTOR_OUT else nc.scalar.copy
                 copy(out=result[:], in_=bank[:])
                 nc.sync.dma_start(out=out_view[i][:, rows[0] : rows[-1] + 1, :], in_=result[:])
 
-        def exists(i):
-            return 0 <= i < UNITS
+        chunk_units = {0: 1, 1: 1, 2: 1, 3: 1}
+        for g in range(2, BLOCKS):
+            chunk_units[2 * g] = 2
+        V, S, G = nc.vector.tensor_copy, nc.scalar.copy, by_gpsimd
+        ctx.enter_context(
+            tc.manual_schedule(
+                engines={
+                    mybir.EngineType.PE,
+                    mybir.EngineType.DVE,
+                    mybir.EngineType.Activation,
+                    mybir.EngineType.Pool,
+                }
+            )
+        )
+        RU, C, RC, U = (RESET, UPDATE), (CAND,), (RESET, CAND), (UPDATE,)
+        GP = 384
+        SC = 224
 
-        chunks = {}
-        for g in range(BLOCKS):
-            units = 1 if g in (0, BLOCKS - 1) else UNITS_PER_BLOCK
-            for i in range(g * UNITS_PER_BLOCK, (g + 1) * UNITS_PER_BLOCK, units):
-                chunks[i] = (i, units)
+        def sigmoids(i):
+            sigmoid(i, RESET)
+            sigmoid(i, UPDATE)
 
-        for t in range(-3, UNITS + 1):
-            if exists(t + 1):
-                sigmoids(t + 1)
-            if t + 2 in chunks:
-                quantise_weights(chunks[t + 2])
-            if exists(t + 2):
-                if (t + 2) % UNITS_PER_BLOCK == 0:
-                    quantise_h((t + 2) // UNITS_PER_BLOCK)
-            if exists(t + 1):
-                gate_candidate(t + 1)
-            if exists(t + 2):
-                multiply(t + 2)
-            if exists(t + 3) and (t + 3) % UNITS_PER_BLOCK == 0:
-                turn_h((t + 3) // UNITS_PER_BLOCK)
-            if exists(t + 1) and t + 1 not in SUBTRACTED:
-                turn_d(t + 1)
-            if exists(t):
-                candidate(t)
-            if exists(t - 1):
-                add_d_and_store(t - 1)
-            if exists(t):
-                blend(t)
-            if exists(t + 3):
-                if (t + 3) % UNITS_PER_BLOCK == 0:
-                    group_h((t + 3) // UNITS_PER_BLOCK)
-                if t + 3 in chunks:
-                    regroup_weights(chunks[t + 3])
+        def unit_weights(i, cand=True):
+            regroup(i, RESET, V)
+            if cand:
+                regroup(i, CAND, V)
+            quantise(i, U)
+            quantise(i, RC)
+
+        def blend_out(i):
+            keep_d(i)
+            blend(i)
+
+        turn_h(0)
+        group_h(0)
+        quantise_h(0)
+        regroup(0, RESET, V)
+        regroup(1, RESET, S)
+        quantise(0, (RESET,))
+        quantise(1, (RESET,))
+        turn_bias()
+        regroup(0, UPDATE, S)
+        regroup(0, CAND, V)
+        regroup(1, CAND, V)
+        quantise(0, U)
+        quantise(0, C)
+        turn_h(1)
+        multiply(0)
+        group_h(1)
+        regroup(1, UPDATE, S)
+        quantise_h(1)
+        quantise(1, C)
+        quantise(1, U)
+        open_d(0)
+        sigmoids(0)
+        gate_candidate(0)
+        multiply(1)
+        open_d(1)
+        regroup(2, UPDATE, S)
+        sigmoids(1)
+        unit_weights(2)
+        candidate(0)
+        gate_candidate(1)
+        multiply(2)
+        turn_h(2)
+        regroup(3, UPDATE, S)
+        candidate(1)
+        subtract(1)
+        sigmoids(2)
+        keep_d(0)
+        blend(0)
+        back(0)
+        unit_weights(3)
+        multiply(3, RU)
+        group_h(2)
+        regroup(4, UPDATE, S)
+        sigmoids(3)
+        back_out(0)
+        regroup(4, RESET, V)
+        regroup(4, CAND, V)
+        quantise_h(2)
+        quantise(4, RC)
+        quantise(4, U)
+        for g in range(1, BLOCKS - 1):
+            a, b = 2 * g, 2 * g + 1
+            n, m = a + 2, a + 4
+            more = g + 2 < BLOCKS
+            if more:
+                regroup(m, UPDATE, G, 0, GP, run=1)
+                regroup(m, UPDATE, S, GP, BLOCK)
+            gate_candidate(a)
+            multiply(n, RU)
+            multiply(b, C)
+            if a - 2 in SUBTRACTED:
+                blend_out(a - 2)
+                back(a - 2)
+            open_d(a)
+            if more:
+                turn_h(g + 2)
+            candidate(a)
+            if more:
+                regroup(m, CAND, S, BLOCK - SC, BLOCK)
+                group_h(g + 2)
+            if a - 2 in SUBTRACTED:
+                back_out(a - 2)
+            sigmoids(n)
+            blend_out(a - 1)
+            gate_candidate(b)
+            multiply(n, C)
+            open_d(b)
+            if a not in SUBTRACTED:
+                blend_out(a)
+            back(a - 1)
+            if a not in SUBTRACTED:
+                back(a)
+            subtract(a)
+            if more:
+                multiply(n + 1, RU)
+            candidate(b)
+            if more:
+                sigmoids(n + 1)
+            subtract(b)
+            if not more:
+                multiply(n + 1, RU)
+            back_out(a - 1)
+            if a not in SUBTRACTED and more:
+                back_out(a)
+            if more:
+                regroup(m, RESET, V)
+                regroup(m, CAND, V, 0, BLOCK - SC)
+                quantise_h(g + 2)
+                quantise(m, RC)
+                quantise(m, U)
+        a, b = UNITS - 2, UNITS - 1
+        gate_candidate(a)
+        keep_d(a - 1)
+        sigmoid(b, RESET)
+        blend(a - 1)
+        candidate(a)
+        sigmoid(b, UPDATE)
+        multiply(b, C)
+        open_d(a)
+        back(a - 1)
+        gate_candidate(b)
+        candidate(b)
+        keep_d(a)
+        blend(a)
+        open_d(b)
+        back(a)
+        keep_d(b)
+        blend(b)
+        back_out(a - 2)
+        back_out(a - 1)
+        back_out(a)
+        back(b)
+        back_out(b)

@@ -26,9 +26,11 @@ UNIT_TILES = UNIT // P
 UNITS = BLOCKS * BLOCK // UNIT
 UNITS_PER_BLOCK = BLOCK // UNIT
 BIAS_TILES = BLOCKS * GATES * BLOCK // P
-SUBTRACTED = [1, 3, 5, 7, 9, 11]
-VECTOR_OUT = (14,)
+SUBTRACTED = [0, 1, 3, 5, 7, 9, 11]
+VECTOR_OUT = ()
 W_BUFS = 7
+CB = 2
+HB = 2
 RUN = 4
 
 FLOPS = 2 * ROWS * BLOCKS * BLOCK * GATES * BLOCK
@@ -78,9 +80,9 @@ def tile_blockrecurrentmodel_pb_kernel(tc, h, d, W_gate, b_gate, out):
                 w_tiles[g, gate] = piece[:, :, (gate - lo) * BLOCK : (gate - lo + 1) * BLOCK]
 
         load_h(0)
-        load_w(0, 0, 1)
+        load_w(0, 0, 2)
         load_bias()
-        load_w(0, 1, 3)
+        load_w(0, 2, 3)
         load_h(1)
         load_w(1)
         load_d(0)
@@ -129,7 +131,7 @@ def tile_blockrecurrentmodel_pb_kernel(tc, h, d, W_gate, b_gate, out):
         def turn_h(g):
             words = h_tiles[g][:].rearrange("p r f -> p (r f)").bitcast(F32)
             words = words.rearrange("p (r q u) -> p r u q", r=ROW_TILES, u=2)
-            turned = psum.tile([P, 2, ROWS], F32, tag="h_turned")
+            turned = psum.tile([P, 2, ROWS], F32, tag="out_turned", bufs=HB)
             for u in range(2):
                 for r in range(ROW_TILES):
                     nc.tensor.transpose(turned[:, u, r * P : (r + 1) * P], words[:, r, u, :], ident_f32[:])
@@ -199,7 +201,7 @@ def tile_blockrecurrentmodel_pb_kernel(tc, h, d, W_gate, b_gate, out):
             g = i // UNITS_PER_BLOCK
             for gate in gates_in:
                 codes, scales, first = w_quantised[i, gate]
-                bank = psum.tile([P, UNIT_TILES, ROWS], F32, tag="ruc"[gate])
+                bank = psum.tile([P, UNIT_TILES, ROWS], F32, tag="ruc"[gate], bufs=CB if gate == CAND else 1)
                 for j in range(UNIT_TILES):
                     lo = first + j * P
                     nc.tensor.matmul_mx(
@@ -350,7 +352,7 @@ def tile_blockrecurrentmodel_pb_kernel(tc, h, d, W_gate, b_gate, out):
         )
         RU, C, RC, U = (RESET, UPDATE), (CAND,), (RESET, CAND), (UPDATE,)
         GP = 384
-        SC = 224
+        SC = 240
 
         def sigmoids(i):
             sigmoid(i, RESET)
@@ -369,45 +371,46 @@ def tile_blockrecurrentmodel_pb_kernel(tc, h, d, W_gate, b_gate, out):
 
         turn_h(0)
         group_h(0)
+        regroup(0, UPDATE, S)
         quantise_h(0)
         regroup(0, RESET, V)
-        regroup(1, RESET, S)
-        quantise(0, (RESET,))
-        quantise(1, (RESET,))
-        turn_bias()
-        regroup(0, UPDATE, S)
-        regroup(0, CAND, V)
-        regroup(1, CAND, V)
-        quantise(0, U)
-        quantise(0, C)
-        turn_h(1)
-        multiply(0)
-        group_h(1)
         regroup(1, UPDATE, S)
+        regroup(1, RESET, V)
+        quantise(0, U)
+        turn_bias()
+        quantise(0, (RESET,))
+        quantise(1, U)
+        quantise(1, (RESET,))
+        turn_h(1)
+        regroup(0, CAND, V)
+        regroup(1, CAND, S)
+        group_h(1)
+        quantise(0, C)
+        multiply(0)
         quantise_h(1)
         quantise(1, C)
-        quantise(1, U)
-        open_d(0)
         sigmoids(0)
         gate_candidate(0)
         multiply(1)
+        open_d(0)
         open_d(1)
         regroup(2, UPDATE, S)
         sigmoids(1)
         unit_weights(2)
         candidate(0)
+        subtract(0)
         gate_candidate(1)
         multiply(2)
         turn_h(2)
         regroup(3, UPDATE, S)
         candidate(1)
-        subtract(1)
         sigmoids(2)
-        keep_d(0)
-        blend(0)
-        back(0)
+        subtract(1)
         unit_weights(3)
-        multiply(3, RU)
+        blend_out(0)
+        open_d(2)
+        back(0)
+        multiply(3)
         group_h(2)
         regroup(4, UPDATE, S)
         sigmoids(3)
@@ -423,43 +426,30 @@ def tile_blockrecurrentmodel_pb_kernel(tc, h, d, W_gate, b_gate, out):
             more = g + 2 < BLOCKS
             if more:
                 regroup(m, UPDATE, G, 0, GP, run=1)
+                turn_h(g + 2)
                 regroup(m, UPDATE, S, GP, BLOCK)
             gate_candidate(a)
-            multiply(n, RU)
-            multiply(b, C)
-            if a - 2 in SUBTRACTED:
-                blend_out(a - 2)
-                back(a - 2)
-            open_d(a)
-            if more:
-                turn_h(g + 2)
+            multiply(n)
             candidate(a)
             if more:
-                regroup(m, CAND, S, BLOCK - SC, BLOCK)
                 group_h(g + 2)
-            if a - 2 in SUBTRACTED:
-                back_out(a - 2)
+                regroup(m, CAND, S, BLOCK - SC, BLOCK)
             sigmoids(n)
             blend_out(a - 1)
+            keep_d(a)
             gate_candidate(b)
-            multiply(n, C)
-            open_d(b)
-            if a not in SUBTRACTED:
-                blend_out(a)
             back(a - 1)
-            if a not in SUBTRACTED:
-                back(a)
-            subtract(a)
-            if more:
-                multiply(n + 1, RU)
+            open_d(b)
+            open_d(n)
+            blend(a)
+            back(a)
+            multiply(n + 1)
             candidate(b)
+            back_out(a - 1)
             if more:
                 sigmoids(n + 1)
             subtract(b)
-            if not more:
-                multiply(n + 1, RU)
-            back_out(a - 1)
-            if a not in SUBTRACTED and more:
+            if more:
                 back_out(a)
             if more:
                 regroup(m, RESET, V)
@@ -473,19 +463,17 @@ def tile_blockrecurrentmodel_pb_kernel(tc, h, d, W_gate, b_gate, out):
         sigmoid(b, RESET)
         blend(a - 1)
         candidate(a)
-        sigmoid(b, UPDATE)
-        multiply(b, C)
-        open_d(a)
         back(a - 1)
+        open_d(b)
+        back_out(a - 2)
+        sigmoid(b, UPDATE)
         gate_candidate(b)
         candidate(b)
         keep_d(a)
         blend(a)
-        open_d(b)
         back(a)
         keep_d(b)
         blend(b)
-        back_out(a - 2)
         back_out(a - 1)
         back_out(a)
         back(b)

@@ -183,6 +183,13 @@ def tile_blockrecurrentmodel_pb_kernel(tc, h, d, W_gate, b_gate, out):
             else:
                 copy(out=place.rearrange("p (c s) t -> p c t s", s=run), in_=src.rearrange("p t (c s) -> p c t s", s=run))
 
+        def V(out, in_):
+            nc.vector.tensor_copy(
+                out=out.rearrange("p (c h) t s -> p h c t s", h=2), in_=in_.rearrange("p (c h) t s -> p h c t s", h=2)
+            )
+
+        S = nc.scalar.copy
+
         def quantise(first_unit, gates_in):
             width = chunk_units[first_unit] * UNIT
             n = len(gates_in) * width
@@ -339,7 +346,7 @@ def tile_blockrecurrentmodel_pb_kernel(tc, h, d, W_gate, b_gate, out):
         chunk_units = {0: 1, 1: 1, 2: 1, 3: 1}
         for g in range(2, BLOCKS):
             chunk_units[2 * g] = 2
-        V, S, G = nc.vector.tensor_copy, nc.scalar.copy, by_gpsimd
+        G = by_gpsimd
         ctx.enter_context(
             tc.manual_schedule(
                 engines={
@@ -351,8 +358,8 @@ def tile_blockrecurrentmodel_pb_kernel(tc, h, d, W_gate, b_gate, out):
             )
         )
         RU, C, RC, U = (RESET, UPDATE), (CAND,), (RESET, CAND), (UPDATE,)
-        GP = 384
-        SC = 240
+        GP = 352
+        SC = 208
 
         def sigmoids(i):
             sigmoid(i, RESET)

@@ -79,12 +79,25 @@ def tile_blockrecurrentmodel_pb_kernel(tc, h, d, W_gate, b_gate, out):
             for gate in range(lo, hi):
                 w_tiles[g, gate] = piece[:, :, (gate - lo) * BLOCK : (gate - lo + 1) * BLOCK]
 
-        load_h(0)
+        def load_half(g, gate, part):
+            piece = const.tile([P, PACK, UNIT], BF16, tag="w_%d_%d_%d" % (g, gate, part))
+            nc.sync.dma_start(
+                out=piece[:], in_=w_view[g][:, :, gate * BLOCK + part * UNIT : gate * BLOCK + (part + 1) * UNIT]
+            )
+            w_tiles[g, gate, part] = piece[:]
+
+        def weight_columns(g, gate, lo, hi):
+            if (g, gate) in w_tiles:
+                return w_tiles[g, gate][:, :, lo:hi]
+            part = lo // UNIT
+            return w_tiles[g, gate, part][:, :, lo - part * UNIT : hi - part * UNIT]
+
         load_w(0, 0, 2)
         load_bias()
+        load_h(0)
         load_w(0, 2, 3)
-        load_h(1)
         load_w(1)
+        load_h(1)
         load_d(0)
         for g in range(2, BLOCKS):
             load_h(g)
@@ -176,19 +189,12 @@ def tile_blockrecurrentmodel_pb_kernel(tc, h, d, W_gate, b_gate, out):
             g, part = divmod(first_unit, UNITS_PER_BLOCK)
             first = part * UNIT
             hi = place.shape[1] if hi is None else hi
-            src = w_tiles[g, gate][:, :, first + lo : first + hi]
+            src = weight_columns(g, gate, first + lo, first + hi)
             place = place[:, lo:hi, :]
             if run == 1:
                 copy(out=place, in_=src.rearrange("p t c -> p c t"))
             else:
                 copy(out=place.rearrange("p (c s) t -> p c t s", s=run), in_=src.rearrange("p t (c s) -> p c t s", s=run))
-
-        def V(out, in_):
-            nc.vector.tensor_copy(
-                out=out.rearrange("p (c h) t s -> p h c t s", h=2), in_=in_.rearrange("p (c h) t s -> p h c t s", h=2)
-            )
-
-        S = nc.scalar.copy
 
         def quantise(first_unit, gates_in):
             width = chunk_units[first_unit] * UNIT
@@ -346,7 +352,7 @@ def tile_blockrecurrentmodel_pb_kernel(tc, h, d, W_gate, b_gate, out):
         chunk_units = {0: 1, 1: 1, 2: 1, 3: 1}
         for g in range(2, BLOCKS):
             chunk_units[2 * g] = 2
-        G = by_gpsimd
+        V, S, G = nc.vector.tensor_copy, nc.scalar.copy, by_gpsimd
         ctx.enter_context(
             tc.manual_schedule(
                 engines={
@@ -358,8 +364,8 @@ def tile_blockrecurrentmodel_pb_kernel(tc, h, d, W_gate, b_gate, out):
             )
         )
         RU, C, RC, U = (RESET, UPDATE), (CAND,), (RESET, CAND), (UPDATE,)
-        GP = 352
-        SC = 208
+        GP = 384
+        SC = 240
 
         def sigmoids(i):
             sigmoid(i, RESET)
@@ -376,37 +382,40 @@ def tile_blockrecurrentmodel_pb_kernel(tc, h, d, W_gate, b_gate, out):
             keep_d(i)
             blend(i)
 
+        regroup(0, UPDATE, S)
+        regroup(0, RESET, V)
         turn_h(0)
         group_h(0)
-        regroup(0, UPDATE, S)
-        quantise_h(0)
-        regroup(0, RESET, V)
         regroup(1, UPDATE, S)
         regroup(1, RESET, V)
         quantise(0, U)
         turn_bias()
         quantise(0, (RESET,))
-        quantise(1, U)
-        quantise(1, (RESET,))
-        turn_h(1)
+        quantise_h(0)
         regroup(0, CAND, V)
-        regroup(1, CAND, S)
-        group_h(1)
+        quantise(1, (RESET,))
         quantise(0, C)
+        regroup(1, CAND, V)
         multiply(0)
-        quantise_h(1)
+        quantise(1, U)
         quantise(1, C)
         sigmoids(0)
-        gate_candidate(0)
         multiply(1)
+        regroup(2, UPDATE, S)
+        turn_h(1)
+        sigmoids(1)
+        group_h(1)
+        regroup(2, RESET, V)
+        gate_candidate(0)
         open_d(0)
         open_d(1)
-        regroup(2, UPDATE, S)
-        sigmoids(1)
-        unit_weights(2)
+        regroup(2, CAND, V)
+        quantise(2, U)
+        quantise(2, RC)
+        gate_candidate(1)
+        quantise_h(1)
         candidate(0)
         subtract(0)
-        gate_candidate(1)
         multiply(2)
         turn_h(2)
         regroup(3, UPDATE, S)
@@ -462,8 +471,8 @@ def tile_blockrecurrentmodel_pb_kernel(tc, h, d, W_gate, b_gate, out):
                 regroup(m, RESET, V)
                 regroup(m, CAND, V, 0, BLOCK - SC)
                 quantise_h(g + 2)
-                quantise(m, RC)
                 quantise(m, U)
+                quantise(m, RC)
         a, b = UNITS - 2, UNITS - 1
         gate_candidate(a)
         keep_d(a - 1)

@@ -196,6 +196,11 @@ def tile_blockrecurrentmodel_pb_kernel(tc, h, d, W_gate, b_gate, out):
             else:
                 copy(out=place.rearrange("p (c s) t -> p c t s", s=run), in_=src.rearrange("p t (c s) -> p c t s", s=run))
 
+        def V(out, in_):
+            nc.vector.tensor_copy(
+                out=out.rearrange("p (c h) t s -> p h c t s", h=2), in_=in_.rearrange("p (c h) t s -> p h c t s", h=2)
+            )
+
         def quantise(first_unit, gates_in):
             width = chunk_units[first_unit] * UNIT
             n = len(gates_in) * width
@@ -352,7 +357,7 @@ def tile_blockrecurrentmodel_pb_kernel(tc, h, d, W_gate, b_gate, out):
         chunk_units = {0: 1, 1: 1, 2: 1, 3: 1}
         for g in range(2, BLOCKS):
             chunk_units[2 * g] = 2
-        V, S, G = nc.vector.tensor_copy, nc.scalar.copy, by_gpsimd
+        S, G = nc.scalar.copy, by_gpsimd
         ctx.enter_context(
             tc.manual_schedule(
                 engines={

@@ -139,7 +139,7 @@ def tile_blockrecurrentmodel_pb_kernel(tc, h, d, W_gate, b_gate, out):
         w_grouped, w_quantised = {}, {}
         gates, d_turned, out_turned = {}, {}, {}
         reset, update, gated, cand = {}, {}, {}, {}
-        kept_of, step_of = {}, {}
+        kept_of, step_of, woven = {}, {}, {}
 
         def turn_h(g):
             words = h_tiles[g][:].rearrange("p r f -> p (r f)").bitcast(F32)
@@ -200,6 +200,24 @@ def tile_blockrecurrentmodel_pb_kernel(tc, h, d, W_gate, b_gate, out):
             nc.vector.tensor_copy(
                 out=out.rearrange("p (c h) t s -> p h c t s", h=2), in_=in_.rearrange("p (c h) t s -> p h c t s", h=2)
             )
+
+        def weave(first_unit, lo):
+            if (first_unit, UPDATE) not in w_grouped:
+                new_update(first_unit)
+            g, part = divmod(first_unit, UNITS_PER_BLOCK)
+            first = part * UNIT + lo
+            bank = psum.tile([P, P, PACK], BF16, tag="out_turned", bufs=2)
+            nc.tensor.matmul(
+                out=bank[:].rearrange("p c t -> p t c"),
+                lhsT=ident_bf16[:],
+                rhs=weight_columns(g, UPDATE, first, first + P),
+                start=True,
+                stop=True,
+            )
+            woven[first_unit] = bank
+
+        def unweave(first_unit, lo):
+            nc.scalar.copy(out=w_grouped[first_unit, UPDATE][:, lo : lo + P, :], in_=woven[first_unit][:])
 
         def quantise(first_unit, gates_in):
             width = chunk_units[first_unit] * UNIT
@@ -370,7 +388,7 @@ def tile_blockrecurrentmodel_pb_kernel(tc, h, d, W_gate, b_gate, out):
         )
         RU, C, RC, U = (RESET, UPDATE), (CAND,), (RESET, CAND), (UPDATE,)
         GP = 384
-        SC = 240
+        SC = 272
 
         def sigmoids(i):
             sigmoid(i, RESET)
@@ -448,13 +466,15 @@ def tile_blockrecurrentmodel_pb_kernel(tc, h, d, W_gate, b_gate, out):
             if more:
                 regroup(m, UPDATE, G, 0, GP, run=1)
                 turn_h(g + 2)
-                regroup(m, UPDATE, S, GP, BLOCK)
             gate_candidate(a)
             multiply(n)
+            if more:
+                weave(m, GP)
             candidate(a)
             if more:
                 group_h(g + 2)
                 regroup(m, CAND, S, BLOCK - SC, BLOCK)
+                unweave(m, GP)
             sigmoids(n)
             blend_out(a - 1)
             keep_d(a)

from contextlib import ExitStack

import concourse.mybir as mybir
from concourse.masks import make_identity

FP8X4 = mybir.dt.float8_e4m3fn_x4
BF16 = mybir.dt.bfloat16
F32 = mybir.dt.float32
U32 = mybir.dt.uint32
U8 = mybir.dt.uint8
ACT = mybir.ActivationFunctionType
ALU = mybir.AluOpType

P = 128
PACK = 4
ROWS = 256
ROW_TILES = ROWS // P
BLOCKS = 8
BLOCK = 512
GATES = 3
RESET = 0
UPDATE = 1
CAND = 2
UNIT = 256
UNIT_TILES = UNIT // P
UNITS = BLOCKS * BLOCK // UNIT
UNITS_PER_BLOCK = BLOCK // UNIT
BIAS_TILES = BLOCKS * GATES * BLOCK // P
SUBTRACTED = [0, 1, 3, 5, 7, 9, 11]
VECTOR_OUT = ()
W_BUFS = 7
CB = 2
HB = 2
RUN = 4

FLOPS = 2 * ROWS * BLOCKS * BLOCK * GATES * BLOCK


def tile_blockrecurrentmodel_pb_kernel(tc, h, d, W_gate, b_gate, out):
    nc = tc.nc

    h_view = h.rearrange("(r p) (g f) -> g p r f", p=P, f=BLOCK)
    d_view = d.flatten_outer_dims().rearrange("(r p) (g f) -> g p r f", p=P, f=BLOCK)
    out_view = out.flatten_outer_dims().rearrange("(r p) (i f) -> i p r f", p=P, f=UNIT)
    w_view = W_gate.rearrange("g (p t) c -> g p t c", t=PACK)
    bias_view = b_gate.rearrange("g (m p) -> (g m) p", p=P)

    with ExitStack() as ctx:
        const = ctx.enter_context(tc.tile_pool(name="const", bufs=1))
        inputs = ctx.enter_context(tc.tile_pool(name="inputs", bufs=BLOCKS))
        stage = ctx.enter_context(tc.tile_pool(name="stage", bufs=3))
        quant = ctx.enter_context(tc.tile_pool(name="quant", bufs=3))
        work = ctx.enter_context(tc.tile_pool(name="work", bufs=2))
        psum = ctx.enter_context(tc.psum_pool(name="psum", bufs=1))

        bias_rows = const.tile([P, P], BF16)
        h_tiles, w_tiles, d_tiles = {}, {}, {}

        def load_bias():
            nc.sync.dma_start(out=bias_rows[0:BIAS_TILES, :], in_=bias_view)

        def load_h(g):
            h_sb = inputs.tile([P, ROW_TILES, BLOCK], BF16, tag="h_sb")
            nc.sync.dma_start(out=h_sb[:], in_=h_view[g])
            h_tiles[g] = h_sb

        def load_d(g):
            d_sb = inputs.tile([P, ROW_TILES, BLOCK], BF16, tag="d_sb")
            nc.sync.dma_start(out=d_sb[:], in_=d_view[g])
            d_tiles[g] = d_sb

        def load_w(g, lo=0, hi=GATES):
            if lo == 0 and hi == GATES:
                piece = inputs.tile([P, PACK, GATES * BLOCK], BF16, tag="w_sb", bufs=W_BUFS)
                nc.sync.dma_start(out=piece[:], in_=w_view[g])
            else:
                piece = const.tile([P, PACK, (hi - lo) * BLOCK], BF16, tag="w_%d_%d" % (g, lo))
                nc.sync.dma_start(out=piece[:], in_=w_view[g][:, :, lo * BLOCK : hi * BLOCK])
            for gate in range(lo, hi):
                w_tiles[g, gate] = piece[:, :, (gate - lo) * BLOCK : (gate - lo + 1) * BLOCK]

        def load_half(g, gate, part):
            piece = const.tile([P, PACK, UNIT], BF16, tag="w_%d_%d_%d" % (g, gate, part))
            nc.sync.dma_start(
                out=piece[:], in_=w_view[g][:, :, gate * BLOCK + part * UNIT : gate * BLOCK + (part + 1) * UNIT]
            )
            w_tiles[g, gate, part] = piece[:]

        def weight_columns(g, gate, lo, hi):
            if (g, gate) in w_tiles:
                return w_tiles[g, gate][:, :, lo:hi]
            part = lo // UNIT
            return w_tiles[g, gate, part][:, :, lo - part * UNIT : hi - part * UNIT]

        load_w(0, 0, 2)
        load_bias()
        load_h(0)
        load_w(0, 2, 3)
        load_w(1)
        load_h(1)
        load_d(0)
        for g in range(2, BLOCKS):
            load_h(g)
            load_w(g)
            load_d(g - 1)
        load_d(BLOCKS - 1)
        ident_f32 = const.tile([P, P], F32)
        make_identity(nc, ident_f32[:])
        negative_ident = const.tile([P, P], F32)
        nc.gpsimd.tensor_scalar(
            out=negative_ident[:], in0=ident_f32[:], scalar1=-1.0, scalar2=0.0, op0=ALU.mult, op1=ALU.add
        )
        ident_bf16 = const.tile([P, P], BF16)
        make_identity(nc, ident_bf16[:])

        zero = const.tile([P, 1], F32)
        nc.vector.memset(zero[:], 0.0)
        warm = const.tile([P, 1], F32)
        nc.scalar.activation(out=warm[:], in_=zero[:], func=ACT.Sigmoid)

        nc.vector.memset(bias_rows[BIAS_TILES:P, :], 0.0)
        bias = const.tile([P, BIAS_TILES], F32)

        def turn_bias():
            bias_turned = psum.tile([P, P], BF16, tag="out_turned", bufs=2)
            nc.tensor.transpose(bias_turned[:], bias_rows[:], ident_bf16[:])
            nc.vector.tensor_copy(out=bias[:], in_=bias_turned[:, 0:BIAS_TILES])
            update_bias = bias[:].rearrange("p (g a q) -> p g a q", g=BLOCKS, a=GATES)[:, :, UPDATE, :]
            nc.vector.tensor_scalar(
                out=update_bias, in0=update_bias, scalar1=-1.0, scalar2=1.0, op0=ALU.mult, op1=ALU.add
            )

        def bias_column(i, gate, j):
            g, part = divmod(i, UNITS_PER_BLOCK)
            col = (g * GATES + gate) * (BLOCK // P) + part * UNIT_TILES + j
            return bias[:, col : col + 1]

        h_turned, h_grouped, h_codes, h_scales = {}, {}, {}, {}
        w_grouped, w_quantised = {}, {}
        gates, d_turned, out_turned = {}, {}, {}
        reset, update, gated, cand = {}, {}, {}, {}
        kept_of, step_of, woven = {}, {}, {}

        def turn_h(g):
            words = h_tiles[g][:].rearrange("p r f -> p (r f)").bitcast(F32)
            words = words.rearrange("p (r q u) -> p r u q", r=ROW_TILES, u=2)
            turned = psum.tile([P, 2, ROWS], F32, tag="out_turned", bufs=HB)
            for u in range(2):
                for r in range(ROW_TILES):
                    nc.tensor.transpose(turned[:, u, r * P : (r + 1) * P], words[:, r, u, :], ident_f32[:])
            h_turned[g] = turned

        def by_gpsimd(out, in_):
            nc.gpsimd.tensor_scalar(out=out, in0=in_, scalar1=1.0, scalar2=0.0, op0=ALU.mult, op1=ALU.add)

        def group_h(g):
            grouped = stage.tile([P, ROWS * PACK], BF16, align_bytes=64, tag="h_grouped")
            nc.scalar.copy(
                out=grouped[:].bitcast(F32).rearrange("p (n u) -> p n u", u=2),
                in_=h_turned[g][:].rearrange("p u n -> p n u"),
            )
            h_grouped[g] = grouped

        def quantise_h(g):
            codes = quant.tile([P, ROWS], U32, align_bytes=64, tag="h_codes")
            scales = quant.tile([P, ROWS], U8, align_bytes=64, tag="h_scales")
            nc.vector.quantize_mx(out=codes[:].bitcast(FP8X4), scales=scales[:], in_=h_grouped[g][:])
            h_codes[g], h_scales[g] = codes, scales

        def new_grouped(first_unit):
            width = chunk_units[first_unit] * UNIT
            main = stage.tile([P, 2 * width, PACK], BF16, align_bytes=64, tag="w_grouped", bufs=2)
            w_grouped[first_unit, RESET] = main[:, 0:width, :]
            w_grouped[first_unit, CAND] = main[:, width : 2 * width, :]
            w_grouped[first_unit] = main

        def new_update(first_unit):
            width = chunk_units[first_unit] * UNIT
            tile = stage.tile([P, width, PACK], BF16, align_bytes=64, tag="u_grouped_%d" % chunk_units[first_unit], bufs=1 if chunk_units[first_unit] > 1 else 2)
            w_grouped[first_unit, UPDATE] = tile[:]

        def regroup(first_unit, gate, copy, lo=0, hi=None, run=RUN):
            if (first_unit, gate) not in w_grouped:
                if gate == UPDATE:
                    new_update(first_unit)
                else:
                    new_grouped(first_unit)
            place = w_grouped[first_unit, gate]
            g, part = divmod(first_unit, UNITS_PER_BLOCK)
            first = part * UNIT
            hi = place.shape[1] if hi is None else hi
            src = weight_columns(g, gate, first + lo, first + hi)
            place = place[:, lo:hi, :]
            if run == 1:
                copy(out=place, in_=src.rearrange("p t c -> p c t"))
            else:
                copy(out=place.rearrange("p (c s) t -> p c t s", s=run), in_=src.rearrange("p t (c s) -> p c t s", s=run))

        def V(out, in_):
            nc.vector.tensor_copy(
                out=out.rearrange("p (c h) t s -> p h c t s", h=2), in_=in_.rearrange("p (c h) t s -> p h c t s", h=2)
            )

        def weave(first_unit, lo):
            if (first_unit, UPDATE) not in w_grouped:
                new_update(first_unit)
            g, part = divmod(first_unit, UNITS_PER_BLOCK)
            first = part * UNIT + lo
            bank = psum.tile([P, P, PACK], BF16, tag="out_turned", bufs=2)
            nc.tensor.matmul(
                out=bank[:].rearrange("p c t -> p t c"),
                lhsT=ident_bf16[:],
                rhs=weight_columns(g, UPDATE, first, first + P),
                start=True,
                stop=True,
            )
            woven[first_unit] = bank

        def unweave(first_unit, lo):
            nc.scalar.copy(out=w_grouped[first_unit, UPDATE][:, lo : lo + P, :], in_=woven[first_unit][:])

        def quantise(first_unit, gates_in):
            width = chunk_units[first_unit] * UNIT
            n = len(gates_in) * width
            name = "".join("ruc"[gate] for gate in gates_in) + "_%d" % chunk_units[first_unit]
            codes = quant.tile([P, n], U32, align_bytes=64, tag="codes_" + name, bufs=2)
            scales = quant.tile([P, n], U8, align_bytes=64, tag="scales_" + name, bufs=2)
            src = w_grouped[first_unit][:] if len(gates_in) == 2 else w_grouped[first_unit, gates_in[0]]
            nc.vector.quantize_mx(
                out=codes[:].bitcast(FP8X4), scales=scales[:], in_=src.rearrange("p w t -> p (w t)")
            )
            for k, gate in enumerate(gates_in):
                for unit in range(chunk_units[first_unit]):
                    w_quantised[first_unit + unit, gate] = (codes, scales, k * width + unit * UNIT)

        def multiply(i, gates_in=(RESET, UPDATE, CAND)):
            g = i // UNITS_PER_BLOCK
            for gate in gates_in:
                codes, scales, first = w_quantised[i, gate]
                bank = psum.tile([P, UNIT_TILES, ROWS], F32, tag="ruc"[gate], bufs=CB if gate == CAND else 1)
                for j in range(UNIT_TILES):
                    lo = first + j * P
                    nc.tensor.matmul_mx(
                        out=bank[:, j, :],
                        lhsT=codes[:, lo : lo + P].bitcast(FP8X4),
                        lhsT_scale=scales[:, lo : lo + P],
                        rhs=h_codes[g][:].bitcast(FP8X4),
                        rhs_scale=h_scales[g][:],
                        start=True,
                        stop=True,
                    )
                gates[i, gate] = bank

        def turn_d(i):
            g, part = divmod(i, UNITS_PER_BLOCK)
            turned = psum.tile([P, UNIT_TILES, ROWS], BF16, tag="d_turned", bufs=2)
            for j in range(UNIT_TILES):
                first = part * UNIT + j * P
                for r in range(ROW_TILES):
                    nc.tensor.transpose(
                        turned[:, j, r * P : (r + 1) * P], d_tiles[g][:, r, first : first + P], ident_bf16[:]
                    )
            d_turned[i] = turned

        def sigmoid(i, gate):
            if gate == RESET:
                act = work.tile([P, UNIT_TILES, ROWS], F32, tag="reset", bufs=3)
                reset[i] = act
            else:
                act = work.tile([P, UNIT_TILES, ROWS], F32, tag="update", bufs=4)
                update[i] = act
            for j in range(UNIT_TILES):
                nc.scalar.activation(
                    out=act[:, j, :],
                    in_=gates[i, gate][:, j, :],
                    func=ACT.Sigmoid,
                    bias=bias_column(i, gate, j),
                    scale=1.0 if gate == RESET else -1.0,
                )

        def gate_candidate(i):
            c_bank = gates[i, CAND]
            gated_sb = work.tile([P, UNIT_TILES, ROWS], F32, tag="gated")
            for j in range(UNIT_TILES):
                nc.vector.scalar_tensor_tensor(
                    out=gated_sb[:, j, :],
                    in0=c_bank[:, j, :],
                    scalar=bias_column(i, CAND, j),
                    in1=reset[i][:, j, :],
                    op0=ALU.add,
                    op1=ALU.mult,
                )
            gated[i] = gated_sb

        def candidate(i):
            cand_sb = work.tile([P, UNIT_TILES, ROWS], F32, tag="cand", bufs=3)
            nc.scalar.activation(
                out=cand_sb[:], in_=gated[i][:], func=ACT.Tanh, scale=1.0 if i in SUBTRACTED else -1.0
            )
            cand[i] = cand_sb

        def open_d(i):
            if i not in SUBTRACTED:
                turn_d(i)
                return
            g, part = divmod(i, UNITS_PER_BLOCK)
            difference = psum.tile([P, UNIT_TILES, ROWS], F32, tag="d_turned", bufs=2)
            for j in range(UNIT_TILES):
                lo = part * UNIT + j * P
                for r in range(ROW_TILES):
                    nc.tensor.matmul(
                        out=difference[:, j, r * P : (r + 1) * P],
                        lhsT=d_tiles[g][:, r, lo : lo + P],
                        rhs=ident_bf16[:],
                        start=(j == 0 and r == 0),
                        stop=False,
                    )
            d_turned[i] = difference

        def subtract(i):
            if i in SUBTRACTED:
                nc.tensor.matmul(
                    out=d_turned[i][:], lhsT=negative_ident[:], rhs=cand[i][:], start=False, stop=True
                )

        def keep_d(i):
            if i in SUBTRACTED:
                kept_of[i] = cand[i]
            else:
                kept = work.tile([P, UNIT_TILES, ROWS], F32, tag="kept")
                nc.vector.tensor_tensor(out=kept[:], in0=update[i][:], in1=d_turned[i][:], op=ALU.mult)
                kept_of[i] = kept

        def blend(i):
            step = work.tile([P, UNIT_TILES, ROWS], F32, tag="step")
            if i in SUBTRACTED:
                nc.vector.tensor_tensor(out=step[:], in0=update[i][:], in1=d_turned[i][:], op=ALU.mult)
            else:
                nc.vector.scalar_tensor_tensor(
                    out=step[:], in0=update[i][:], scalar=-1.0, in1=cand[i][:], op0=ALU.add, op1=ALU.mult
                )
            step_of[i] = step

        def back(i):
            groups = ((0,), (1,)) if i == UNITS - 1 else ((0, 1),)
            turned = {}
            for rows in groups:
                bank = psum.tile([P, len(rows), UNIT], F32, tag="out_turned", bufs=2)
                turned[rows] = bank
            for term in (kept_of[i], step_of[i]):
                for rows in groups:
                    for r in rows:
                        for j in range(UNIT_TILES):
                            nc.tensor.matmul(
                                out=turned[rows][:, r - rows[0], j * P : (j + 1) * P],
                                lhsT=term[:, j, r * P : (r + 1) * P],
                                rhs=ident_f32[:],
                                is_transpose=True,
                                start=(term is kept_of[i] and r == rows[0] and j == 0),
                                stop=(term is step_of[i] and r == rows[-1] and j == UNIT_TILES - 1),
                            )
            out_turned[i] = turned

        def back_out(i):
            if 0 <= i < UNITS:
                add_d_and_store(i)

        def add_d_and_store(i):
            for rows, bank in out_turned[i].items():
                result = work.tile([P, len(rows), UNIT], F32, tag="result", bufs=6)
                copy = nc.vector.tensor_copy if rows == (1,) or i in VECTOR_OUT else nc.scalar.copy
                copy(out=result[:], in_=bank[:])
                nc.sync.dma_start(out=out_view[i][:, rows[0] : rows[-1] + 1, :], in_=result[:])

        chunk_units = {0: 1, 1: 1, 2: 1, 3: 1}
        for g in range(2, BLOCKS):
            chunk_units[2 * g] = 2
        S, G = nc.scalar.copy, by_gpsimd
        ctx.enter_context(
            tc.manual_schedule(
                engines={
                    mybir.EngineType.PE,
                    mybir.EngineType.DVE,
                    mybir.EngineType.Activation,
                    mybir.EngineType.Pool,
                }
            )
        )
        RU, C, RC, U = (RESET, UPDATE), (CAND,), (RESET, CAND), (UPDATE,)
        GP = 384
        SC = 272

        def sigmoids(i):
            sigmoid(i, RESET)
            sigmoid(i, UPDATE)

        def unit_weights(i, cand=True):
            regroup(i, RESET, V)
            if cand:
                regroup(i, CAND, V)
            quantise(i, U)
            quantise(i, RC)

        def blend_out(i):
            keep_d(i)
            blend(i)

        regroup(0, UPDATE, S)
        regroup(0, RESET, V)
        turn_h(0)
        group_h(0)
        regroup(1, UPDATE, S)
        regroup(1, RESET, V)
        quantise(0, U)
        turn_bias()
        quantise(0, (RESET,))
        quantise_h(0)
        regroup(0, CAND, V)
        quantise(1, (RESET,))
        quantise(0, C)
        regroup(1, CAND, V)
        multiply(0)
        quantise(1, U)
        quantise(1, C)
        sigmoids(0)
        multiply(1)
        regroup(2, UPDATE, S)
        turn_h(1)
        sigmoids(1)
        group_h(1)
        regroup(2, RESET, V)
        gate_candidate(0)
        open_d(0)
        open_d(1)
        regroup(2, CAND, V)
        quantise(2, U)
        quantise(2, RC)
        gate_candidate(1)
        quantise_h(1)
        candidate(0)
        subtract(0)
        multiply(2)
        turn_h(2)
        regroup(3, UPDATE, S)
        candidate(1)
        sigmoids(2)
        subtract(1)
        unit_weights(3)
        blend_out(0)
        open_d(2)
        back(0)
        multiply(3)
        group_h(2)
        regroup(4, UPDATE, S)
        sigmoids(3)
        back_out(0)
        regroup(4, RESET, V)
        regroup(4, CAND, V)
        quantise_h(2)
        quantise(4, RC)
        quantise(4, U)
        for g in range(1, BLOCKS - 1):
            a, b = 2 * g, 2 * g + 1
            n, m = a + 2, a + 4
            more = g + 2 < BLOCKS
            if more:
                regroup(m, UPDATE, G, 0, GP, run=1)
                turn_h(g + 2)
            gate_candidate(a)
            multiply(n)
            if more:
                weave(m, GP)
            candidate(a)
            if more:
                group_h(g + 2)
                regroup(m, CAND, S, BLOCK - SC, BLOCK)
                unweave(m, GP)
            sigmoids(n)
            blend_out(a - 1)
            keep_d(a)
            gate_candidate(b)
            back(a - 1)
            open_d(b)
            open_d(n)
            blend(a)
            back(a)
            multiply(n + 1)
            candidate(b)
            back_out(a - 1)
            if more:
                sigmoids(n + 1)
            subtract(b)
            if more:
                back_out(a)
            if more:
                regroup(m, RESET, V)
                regroup(m, CAND, V, 0, BLOCK - SC)
                quantise_h(g + 2)
                quantise(m, U)
                quantise(m, RC)
        a, b = UNITS - 2, UNITS - 1
        gate_candidate(a)
        keep_d(a - 1)
        sigmoid(b, RESET)
        blend(a - 1)
        candidate(a)
        back(a - 1)
        open_d(b)
        back_out(a - 2)
        sigmoid(b, UPDATE)
        gate_candidate(b)
        candidate(b)
        keep_d(a)
        blend(a)
        back(a)
        keep_d(b)
        blend(b)
        back_out(a - 1)
        back_out(a)
        back(b)
        back_out(b)
